import numpy as np
import ml_dtypes


def mxq(x, axis, fmt="e4m3"):
    dtype, down = {"e4m3": (ml_dtypes.float8_e4m3fn, 7), "e5m2": (ml_dtypes.float8_e5m2, 14)}[fmt]
    v = np.moveaxis(np.asarray(x, np.float32).astype(ml_dtypes.bfloat16).astype(np.float64), axis, -1)
    blocks = v.reshape(v.shape[:-1] + (-1, 32))
    amax = np.abs(blocks).max(-1, keepdims=True)
    byte = np.maximum(np.where(amax > 0, np.frexp(amax)[1] - 1 + 127, 0) - down, 1)
    scale = np.exp2(byte - 127.0)
    codes = (blocks / scale).astype(np.float32).astype(dtype).astype(np.float64)
    return np.moveaxis((codes * scale).reshape(v.shape), -1, axis)


WIDE = False


def mx_kscale(k):
    if not WIDE:
        return np.ones(k)
    levels = np.array([10, -10, 5, -5, 0])
    if k % 512:
        return np.exp2(np.random.permutation(np.resize(levels, k // 32))).repeat(32)
    a = np.empty((k // 512, 16))
    for p in range(k // 512):
        a[p, :8] = np.random.permutation(np.resize(levels, 8))
        for g in range(8):
            far = levels[np.abs(levels - a[p, g]) >= 10]
            a[p, g + 8] = far[np.random.randint(len(far))]
    return np.exp2(a.ravel()).repeat(32)


BF16 = ml_dtypes.bfloat16


def bf(x):
    return np.asarray(x, np.float32).astype(BF16)


def f64(x):
    return np.asarray(x).astype(np.float64)


B, S, D, E, HD = 2, 512, 512, 512, 64
ROPE_BASE = 10000.0


def rope_tables():
    inv_freq = 1.0 / ROPE_BASE ** (np.arange(0, E, 2) / E)
    ang = np.repeat(np.arange(S)[:, None] * inv_freq[None, :], 2, axis=-1)
    return np.cos(ang), np.sin(ang)


def rotate_half(v):
    h = v.shape[-1] // 2
    return np.concatenate([-v[..., h:], v[..., :h]], axis=-1)


def setup_inputs():
    s = mx_kscale(D)
    return {"x": bf(np.random.standard_normal((B, S, D)) * s),
            "Wq": bf(np.random.standard_normal((D, E)) * 0.5 / np.sqrt(D) / s[:, None]),
            "bq": bf(np.random.standard_normal(E) * 0.1),
            "Wk": bf(np.random.standard_normal((D, E)) * 0.5 / np.sqrt(D) / s[:, None]),
            "bk": bf(np.random.standard_normal(E) * 0.1)}


def reference(x, Wq, bq, Wk, bk):
    xq = mxq(f64(x), 2, "e4m3")
    q = (xq @ mxq(f64(Wq), 0, "e4m3")) + f64(bq)
    k = (xq @ mxq(f64(Wk), 0, "e4m3")) + f64(bk)
    cos, sin = rope_tables()
    qr = q * cos + rotate_half(q) * sin
    kr = k * cos + rotate_half(k) * sin
    return qr, kr

@@ -1,0 +1,315 @@
+import math
+from contextlib import ExitStack
+
+import concourse.mybir as mybir
+from concourse.masks import make_identity
+
+F32 = mybir.dt.float32
+BF16 = mybir.dt.bfloat16
+U32 = mybir.dt.uint32
+U8 = mybir.dt.uint8
+FP8X4 = mybir.dt.float8_e4m3fn_x4
+ALU = mybir.AluOpType
+ACT = mybir.ActivationFunctionType
+
+P = 128
+PACK = 4
+BATCH = 2
+SEQ = 512
+DIM = 512
+FEAT = 512
+PROJECTIONS = 2
+TOKEN_TILES = SEQ // P
+TOKEN_PAIRS = TOKEN_TILES // 2
+HALVES = 2
+HALF = FEAT // HALVES
+PARITIES = 2
+FREQS = FEAT // 2
+COS = 0
+SIN = 1
+ROPE_BASE = 10000.0
+RATIO = ROPE_BASE ** (-1.0 / FREQS)
+TURNS_PER_RADIAN = 1.0 / (2.0 * math.pi)
+ROUND_MAGIC = 1.5 * 2.0**23
+
+FLOPS = 2 * BATCH * SEQ * DIM * PROJECTIONS * FEAT
+
+
+def tile_ropemultiheadattention_pa_kernel(tc, x, Wq, bq, Wk, bk, out_0, out_1):
+    nc = tc.nc
+    weights = (Wq, Wk)
+    biases = (bq, bk)
+    outs = (out_0, out_1)
+
+    with ExitStack() as ctx:
+        keep = ctx.enter_context(tc.tile_pool(name="keep", bufs=1))
+        products = ctx.enter_context(tc.tile_pool(name="products", bufs=8))
+        results = ctx.enter_context(tc.tile_pool(name="results", bufs=6))
+        proj_psum = ctx.enter_context(tc.psum_pool(name="proj_psum", bufs=4))
+        flip_psum = ctx.enter_context(tc.psum_pool(name="flip_psum", bufs=4))
+        ctx.enter_context(tc.manual_schedule())
+
+
+        x_raw = keep.tile([P, BATCH, TOKEN_TILES, DIM], BF16)
+        w_raw = keep.tile([P, PROJECTIONS, PACK, FEAT], BF16)
+
+        def load_x(b):
+            nc.sync.dma_start(
+                out=x_raw[:, b], in_=x[b].rearrange("(c r) k -> c r k", r=TOKEN_TILES)
+            )
+
+        def load_w(w):
+            nc.sync.dma_start(
+                out=w_raw[:, w], in_=weights[w].rearrange("(p t) i -> p t i", t=PACK)
+            )
+
+        identity = keep.tile([P, P], F32)
+        x_flip = {}
+        x_grouped = keep.tile([P, BATCH, TOKEN_TILES, P, PACK], BF16, align_bytes=64)
+        x_codes = keep.tile([P, BATCH, SEQ], U32, align_bytes=64)
+        x_scales = keep.tile([P, BATCH, SEQ], U8, align_bytes=64)
+
+        def transpose_x(b):
+            x_words = x_raw[:, b].bitcast(F32)
+            for pair in range(TOKEN_PAIRS):
+                x_flip[b, pair] = flip_psum.tile([P, 2, 2, P], F32, tag="flip", name="x_flip")
+                for r2 in range(2):
+                    for u in range(2):
+                        nc.tensor.transpose(
+                            x_flip[b, pair][:, r2, u, :],
+                            x_words[:, 2 * pair + r2, u::2],
+                            identity[:],
+                        )
+
+        def group_x(b):
+            for pair in range(TOKEN_PAIRS):
+                nc.scalar.copy(
+                    out=x_grouped[:, b, 2 * pair : 2 * pair + 2, :, :].bitcast(F32),
+                    in_=x_flip[b, pair][:].rearrange("p r u c -> p r c u"),
+                )
+
+        def quantise_x(b):
+            nc.vector.quantize_mx(
+                out=x_codes[:, b, :].bitcast(FP8X4),
+                scales=x_scales[:, b, :],
+                in_=x_grouped[:, b].rearrange("p r c t -> p (r c t)"),
+            )
+
+        w_grouped = keep.tile([P, PROJECTIONS, HALVES, PARITIES, P, PACK], BF16, align_bytes=64)
+        w_codes = keep.tile([P, PROJECTIONS, FEAT], U32, align_bytes=64)
+        w_scales = keep.tile([P, PROJECTIONS, FEAT], U8, align_bytes=64)
+
+        def group_w(w):
+            by_parity = w_raw[:, w].rearrange("p t (h m e) -> p e h m t", h=HALVES, e=PARITIES)
+            for e in range(PARITIES):
+                nc.scalar.copy(out=w_grouped[:, w, :, e, :, :], in_=by_parity[:, e])
+
+        def quantise_w(w):
+            nc.vector.quantize_mx(
+                out=w_codes[:, w, :].bitcast(FP8X4),
+                scales=w_scales[:, w, :],
+                in_=w_grouped[:, w].rearrange("p h e m t -> p (h e m t)"),
+            )
+
+        token = keep.tile([P, TOKEN_TILES, P], F32)
+        freq = keep.tile([P, HALVES], F32)
+        half_pi = keep.tile([P, 1], F32)
+        turns = keep.tile([P, HALVES, SEQ], F32)
+        whole = keep.tile([P, HALVES, SEQ], F32)
+        excess = keep.tile([P, HALVES, SEQ], F32)
+        size = keep.tile([P, HALVES, SEQ], F32)
+        tables = keep.tile([P, HALVES, 2, SEQ], F32)
+
+        def angle_in_turns(h):
+            nc.vector.tensor_scalar_mul(
+                out=turns[:, h, :],
+                in0=token[:].rearrange("p r c -> p (r c)"),
+                scalar1=freq[:, h : h + 1],
+            )
+
+        def round_turns(h):
+            nc.vector.tensor_scalar(
+                out=whole[:, h, :],
+                in0=turns[:, h, :],
+                scalar1=ROUND_MAGIC,
+                scalar2=ROUND_MAGIC,
+                op0=ALU.add,
+                op1=ALU.subtract,
+            )
+
+        def excess_of_turns(h):
+            nc.vector.tensor_sub(out=excess[:, h, :], in0=whole[:, h, :], in1=turns[:, h, :])
+
+        def size_of_excess(h):
+            nc.vector.scalar_tensor_tensor(
+                out=size[:, h, :],
+                in0=excess[:, h, :],
+                scalar=-1.0,
+                in1=excess[:, h, :],
+                op0=ALU.mult,
+                op1=ALU.max,
+            )
+
+        def sin_table(h):
+            nc.scalar.activation(
+                out=tables[:, h, SIN, :],
+                in_=excess[:, h, :],
+                func=ACT.Sin,
+                scale=(2.0 if h == 0 else -2.0) * math.pi,
+            )
+
+        def cos_table(h):
+            nc.scalar.activation(
+                out=tables[:, h, COS, :],
+                in_=size[:, h, :],
+                func=ACT.Sin,
+                scale=-2.0 * math.pi,
+                bias=half_pi[:],
+            )
+
+        bias = []
+        quantised = set()
+
+        def multiply(w, b, e):
+            if ("w", w) not in quantised:
+                quantise_w(w)
+                quantised.add(("w", w))
+            if ("x", b) not in quantised:
+                quantise_x(b)
+                quantised.add(("x", b))
+            proj = []
+            for h in range(HALVES):
+                tile_cols = slice((h * PARITIES + e) * P, (h * PARITIES + e + 1) * P)
+                proj.append(proj_psum.tile([P, SEQ], F32, tag="proj", name="proj"))
+                nc.tensor.matmul_mx(
+                    out=proj[h][:],
+                    lhsT=w_codes[:, w, tile_cols].bitcast(FP8X4),
+                    lhsT_scale=w_scales[:, w, tile_cols],
+                    rhs=x_codes[:, b, :].bitcast(FP8X4),
+                    rhs_scale=x_scales[:, b, :],
+                    start=True,
+                    stop=True,
+                )
+            return proj
+
+        def rotate(w, e, h, proj, back):
+            summands = []
+            for source, kind in ((1 - h, SIN), (h, COS)):
+                product = products.tile([P, SEQ], F32, tag="product")
+                nc.vector.scalar_tensor_tensor(
+                    out=product[:],
+                    in0=proj[source][:],
+                    scalar=bias[w][:, source, e : e + 1],
+                    in1=tables[:, h, kind, :],
+                    op0=ALU.add,
+                    op1=ALU.mult,
+                )
+                summands.append(product)
+            for r in range(TOKEN_TILES):
+                for product in summands:
+                    nc.tensor.matmul(
+                        out=back[h, r // 2][:, r % 2, e, :],
+                        lhsT=product[:, r * P : (r + 1) * P],
+                        rhs=identity[:],
+                        is_transpose=True,
+                        start=product is summands[0],
+                        stop=product is summands[-1],
+                    )
+
+        def store(w, b, h, back):
+            for pair in range(TOKEN_PAIRS):
+                rotated = results.tile([P, 2, HALF], F32)
+                nc.scalar.copy(
+                    out=rotated[:].rearrange("c r (m e) -> c r m e", e=PARITIES),
+                    in_=back[h, pair][:].rearrange("c r e m -> c r m e"),
+                )
+                nc.sync.dma_start(
+                    out=outs[w][b].rearrange("(c r) i -> c r i", r=TOKEN_TILES)[
+                        :, 2 * pair : 2 * pair + 2, h * HALF : (h + 1) * HALF
+                    ],
+                    in_=rotated[:],
+                )
+
+
+        load_w(0)
+        load_x(0)
+        load_x(1)
+        load_w(1)
+
+        bias_bf16 = []
+        for w in range(PROJECTIONS):
+            bias_bf16.append(keep.tile([P, HALVES, PARITIES], BF16, name="bias_bf16_%d" % w))
+            nc.scalar.dma_start(
+                out=bias_bf16[w][:],
+                in_=biases[w].rearrange("(h m e) -> m h e", h=HALVES, e=PARITIES),
+            )
+
+        zero = keep.tile([P, 1], F32)
+        warm = keep.tile([P, 1], F32)
+        nc.vector.memset(zero[:], 0.0)
+        nc.scalar.activation(out=warm[:], in_=zero[:], func=ACT.Sin)
+
+        make_identity(nc, identity[:])
+        nc.gpsimd.iota(
+            token[:],
+            pattern=[[1, TOKEN_TILES], [TOKEN_TILES, P]],
+            base=0,
+            channel_multiplier=0,
+            allow_small_or_imprecise_dtypes=True,
+        )
+        for w in range(PROJECTIONS):
+            bias.append(keep.tile([P, HALVES, PARITIES], F32, name="bias%d" % w))
+            nc.gpsimd.tensor_copy(out=bias[w][:], in_=bias_bf16[w][:])
+
+        freq_row = keep.tile([P, FREQS], F32)
+        nc.vector.memset(freq_row[:, 0:1], 1.0)
+        done = 1
+        while done < FREQS:
+            nc.vector.tensor_scalar_mul(
+                out=freq_row[:, done : 2 * done], in0=freq_row[:, 0:done], scalar1=RATIO**done
+            )
+            done *= 2
+        nc.vector.tensor_scalar_add(out=half_pi[:], in0=zero[:], scalar1=math.pi / 2.0)
+
+        freq_flip = flip_psum.tile([P, HALVES, P], F32, tag="flip")
+        for h in range(HALVES):
+            nc.tensor.transpose(freq_flip[:, h, :], freq_row[:, h * P : (h + 1) * P], identity[:])
+        nc.vector.tensor_scalar_mul(out=freq[:], in0=freq_flip[:, :, 0], scalar1=TURNS_PER_RADIAN)
+
+        group_w(0)
+        transpose_x(0)
+        transpose_x(1)
+        group_x(0)
+        for table_step in (angle_in_turns, round_turns, excess_of_turns):
+            for h in range(HALVES):
+                table_step(h)
+        size_of_excess(0)
+        sin_table(0)
+        cos_table(0)
+        steps = [
+            (w, b, e)
+            for w in range(PROJECTIONS)
+            for b in range(BATCH)
+            for e in range(PARITIES)
+        ]
+        ahead = multiply(*steps[0])
+        size_of_excess(1)
+        sin_table(1)
+        cos_table(1)
+        group_x(1)
+        group_w(1)
+
+        back = {}
+        for step, (w, b, e) in enumerate(steps):
+            proj = ahead
+            if step + 1 < len(steps):
+                ahead = multiply(*steps[step + 1])
+            for h in range(HALVES):
+                if e == 0:
+                    for pair in range(TOKEN_PAIRS):
+                        back[h, pair] = flip_psum.tile(
+                            [P, 2, PARITIES, P], F32, tag="flip", name="back"
+                        )
+                rotate(w, e, h, proj, back)
+                if e == PARITIES - 1:
+                    store(w, b, h, back)

@@ -28,7 +28,6 @@ FREQS = FEAT // 2
 COS = 0
 SIN = 1
 ROPE_BASE = 10000.0
-RATIO = ROPE_BASE ** (-1.0 / FREQS)
 TURNS_PER_RADIAN = 1.0 / (2.0 * math.pi)
 ROUND_MAGIC = 1.5 * 2.0**23
 
@@ -53,9 +52,10 @@ def tile_ropemultiheadattention_pa_kernel(tc, x, Wq, bq, Wk, bk, out_0, out_1):
         x_raw = keep.tile([P, BATCH, TOKEN_TILES, DIM], BF16)
         w_raw = keep.tile([P, PROJECTIONS, PACK, FEAT], BF16)
 
-        def load_x(b):
+        def load_x(b, tiles):
             nc.sync.dma_start(
-                out=x_raw[:, b], in_=x[b].rearrange("(c r) k -> c r k", r=TOKEN_TILES)
+                out=x_raw[:, b, tiles, :],
+                in_=x[b].rearrange("(c r) k -> c r k", r=TOKEN_TILES)[:, tiles, :],
             )
 
         def load_w(w):
@@ -81,106 +81,135 @@ def tile_ropemultiheadattention_pa_kernel(tc, x, Wq, bq, Wk, bk, out_0, out_1):
                             identity[:],
                         )
 
-        def group_x(b):
-            for pair in range(TOKEN_PAIRS):
-                nc.scalar.copy(
-                    out=x_grouped[:, b, 2 * pair : 2 * pair + 2, :, :].bitcast(F32),
-                    in_=x_flip[b, pair][:].rearrange("p r u c -> p r c u"),
-                )
-
-        def quantise_x(b):
-            nc.vector.quantize_mx(
-                out=x_codes[:, b, :].bitcast(FP8X4),
-                scales=x_scales[:, b, :],
-                in_=x_grouped[:, b].rearrange("p r c t -> p (r c t)"),
+        def group_x(b, pair):
+            nc.scalar.copy(
+                out=x_grouped[:, b, 2 * pair : 2 * pair + 2, :, :].bitcast(F32),
+                in_=x_flip[b, pair][:].rearrange("p r u c -> p r c u"),
             )
 
-        w_grouped = keep.tile([P, PROJECTIONS, HALVES, PARITIES, P, PACK], BF16, align_bytes=64)
+        def quantise_x(b, tiles):
+            tokens = slice(tiles.start * P, tiles.stop * P)
+            nc.vector.quantize_mx(
+                out=x_codes[:, b, tokens].bitcast(FP8X4),
+                scales=x_scales[:, b, tokens],
+                in_=x_grouped[:, b, tiles].rearrange("p r c t -> p (r c t)"),
+            )
+
+        w_grouped = keep.tile([P, PROJECTIONS, PARITIES, HALVES, P, PACK], BF16, align_bytes=64)
         w_codes = keep.tile([P, PROJECTIONS, FEAT], U32, align_bytes=64)
         w_scales = keep.tile([P, PROJECTIONS, FEAT], U8, align_bytes=64)
 
-        def group_w(w):
+        def group_w(copy, w, e):
             by_parity = w_raw[:, w].rearrange("p t (h m e) -> p e h m t", h=HALVES, e=PARITIES)
-            for e in range(PARITIES):
-                nc.scalar.copy(out=w_grouped[:, w, :, e, :, :], in_=by_parity[:, e])
+            copy(out=w_grouped[:, w, e], in_=by_parity[:, e])
 
-        def quantise_w(w):
+        def quantise_w(w, e):
+            columns = slice(e * HALF, (e + 1) * HALF)
             nc.vector.quantize_mx(
-                out=w_codes[:, w, :].bitcast(FP8X4),
-                scales=w_scales[:, w, :],
-                in_=w_grouped[:, w].rearrange("p h e m t -> p (h e m t)"),
+                out=w_codes[:, w, columns].bitcast(FP8X4),
+                scales=w_scales[:, w, columns],
+                in_=w_grouped[:, w, e].rearrange("p h m t -> p (h m t)"),
             )
 
         token = keep.tile([P, TOKEN_TILES, P], F32)
         freq = keep.tile([P, HALVES], F32)
+        minus_freq = keep.tile([P, 1], F32)
+        half_freq = keep.tile([P, 1], F32)
         half_pi = keep.tile([P, 1], F32)
-        turns = keep.tile([P, HALVES, SEQ], F32)
-        whole = keep.tile([P, HALVES, SEQ], F32)
-        excess = keep.tile([P, HALVES, SEQ], F32)
-        size = keep.tile([P, HALVES, SEQ], F32)
+        whole_pi = keep.tile([P, 1], F32)
+        turns = keep.tile([P, SEQ], F32)
+        whole = keep.tile([P, SEQ], F32)
+        excess = keep.tile([P, SEQ], F32)
+        size = keep.tile([P, SEQ], F32)
+        half_sin = keep.tile([P, SEQ], F32)
+        half_sin_squared = keep.tile([P, SEQ], F32)
         tables = keep.tile([P, HALVES, 2, SEQ], F32)
+        tokens_in_row = token[:].rearrange("p r c -> p (r c)")
 
-        def angle_in_turns(h):
-            nc.vector.tensor_scalar_mul(
-                out=turns[:, h, :],
-                in0=token[:].rearrange("p r c -> p (r c)"),
-                scalar1=freq[:, h : h + 1],
-            )
-
-        def round_turns(h):
+        def lower_angles():
             nc.vector.tensor_scalar(
-                out=whole[:, h, :],
-                in0=turns[:, h, :],
+                out=turns[:],
+                in0=tokens_in_row,
+                scalar1=freq[:, 0:1],
+                scalar2=TURNS_PER_RADIAN,
+                op0=ALU.mult,
+                op1=ALU.mult,
+            )
+            nc.vector.tensor_scalar(
+                out=whole[:],
+                in0=turns[:],
                 scalar1=ROUND_MAGIC,
                 scalar2=ROUND_MAGIC,
                 op0=ALU.add,
                 op1=ALU.subtract,
             )
+            nc.vector.tensor_sub(out=excess[:], in0=whole[:], in1=turns[:])
 
-        def excess_of_turns(h):
-            nc.vector.tensor_sub(out=excess[:, h, :], in0=whole[:, h, :], in1=turns[:, h, :])
-
-        def size_of_excess(h):
+        def lower_sizes():
             nc.vector.scalar_tensor_tensor(
-                out=size[:, h, :],
-                in0=excess[:, h, :],
+                out=size[:],
+                in0=excess[:],
                 scalar=-1.0,
-                in1=excess[:, h, :],
+                in1=excess[:],
                 op0=ALU.mult,
                 op1=ALU.max,
             )
 
-        def sin_table(h):
+        def lower_sin():
             nc.scalar.activation(
-                out=tables[:, h, SIN, :],
-                in_=excess[:, h, :],
-                func=ACT.Sin,
-                scale=(2.0 if h == 0 else -2.0) * math.pi,
+                out=tables[:, 0, SIN, :], in_=excess[:], func=ACT.Sin, scale=2.0 * math.pi
             )
 
-        def cos_table(h):
+        def lower_cos():
             nc.scalar.activation(
-                out=tables[:, h, COS, :],
-                in_=size[:, h, :],
+                out=tables[:, 0, COS, :],
+                in_=size[:],
                 func=ACT.Sin,
                 scale=-2.0 * math.pi,
                 bias=half_pi[:],
             )
 
+        def upper_half_sin():
+            nc.scalar.activation(
+                out=half_sin[:], in_=tokens_in_row, func=ACT.Sin, scale=half_freq[:]
+            )
+
+        def upper_sin():
+            nc.scalar.activation(
+                out=tables[:, 1, SIN, :],
+                in_=tokens_in_row,
+                func=ACT.Sin,
+                scale=minus_freq[:],
+                bias=whole_pi[:],
+            )
+
+        def upper_cos():
+            nc.gpsimd.tensor_mul(out=half_sin_squared[:], in0=half_sin[:], in1=half_sin[:])
+            nc.gpsimd.tensor_scalar(
+                out=tables[:, 1, COS, :],
+                in0=half_sin_squared[:],
+                scalar1=-2.0,
+                scalar2=1.0,
+                op0=ALU.mult,
+                op1=ALU.add,
+            )
+
         bias = []
         quantised = set()
 
+        def prepare(w, b, e):
+            if (w, e) not in quantised:
+                quantise_w(w, e)
+                quantised.add((w, e))
+            if b not in quantised:
+                quantise_x(b, slice(0, TOKEN_TILES))
+                quantised.add(b)
+
         def multiply(w, b, e):
-            if ("w", w) not in quantised:
-                quantise_w(w)
-                quantised.add(("w", w))
-            if ("x", b) not in quantised:
-                quantise_x(b)
-                quantised.add(("x", b))
-            proj = []
-            for h in range(HALVES):
-                tile_cols = slice((h * PARITIES + e) * P, (h * PARITIES + e + 1) * P)
-                proj.append(proj_psum.tile([P, SEQ], F32, tag="proj", name="proj"))
+            proj = {}
+            for h in reversed(range(HALVES)):
+                tile_cols = slice((e * HALVES + h) * P, (e * HALVES + h + 1) * P)
+                proj[h] = proj_psum.tile([P, SEQ], F32, tag="proj", name="proj")
                 nc.tensor.matmul_mx(
                     out=proj[h][:],
                     lhsT=w_codes[:, w, tile_cols].bitcast(FP8X4),
@@ -192,20 +221,21 @@ def tile_ropemultiheadattention_pa_kernel(tc, x, Wq, bq, Wk, bk, out_0, out_1):
                 )
             return proj
 
-        def rotate(w, e, h, proj, back):
+        def rotate(w, e, h, tiles, proj, back):
+            tokens = slice(tiles.start * P, tiles.stop * P)
             summands = []
             for source, kind in ((1 - h, SIN), (h, COS)):
                 product = products.tile([P, SEQ], F32, tag="product")
                 nc.vector.scalar_tensor_tensor(
-                    out=product[:],
-                    in0=proj[source][:],
+                    out=product[:, tokens],
+                    in0=proj[source][:, tokens],
                     scalar=bias[w][:, source, e : e + 1],
-                    in1=tables[:, h, kind, :],
+                    in1=tables[:, h, kind, tokens],
                     op0=ALU.add,
                     op1=ALU.mult,
                 )
                 summands.append(product)
-            for r in range(TOKEN_TILES):
+            for r in range(tiles.start, tiles.stop):
                 for product in summands:
                     nc.tensor.matmul(
                         out=back[h, r // 2][:, r % 2, e, :],
@@ -216,24 +246,26 @@ def tile_ropemultiheadattention_pa_kernel(tc, x, Wq, bq, Wk, bk, out_0, out_1):
                         stop=product is summands[-1],
                     )
 
-        def store(w, b, h, back):
-            for pair in range(TOKEN_PAIRS):
-                rotated = results.tile([P, 2, HALF], F32)
-                nc.scalar.copy(
-                    out=rotated[:].rearrange("c r (m e) -> c r m e", e=PARITIES),
-                    in_=back[h, pair][:].rearrange("c r e m -> c r m e"),
-                )
-                nc.sync.dma_start(
-                    out=outs[w][b].rearrange("(c r) i -> c r i", r=TOKEN_TILES)[
-                        :, 2 * pair : 2 * pair + 2, h * HALF : (h + 1) * HALF
-                    ],
-                    in_=rotated[:],
-                )
+        def store(copy, w, b, h, pair, back):
+            rotated = results.tile([P, 2, HALF], F32)
+            copy(
+                out=rotated[:].rearrange("c r (m e) -> c r m e", e=PARITIES),
+                in_=back[h, pair][:].rearrange("c r e m -> c r m e"),
+            )
+            nc.sync.dma_start(
+                out=outs[w][b].rearrange("(c r) i -> c r i", r=TOKEN_TILES)[
+                    :, pair_tiles[pair], h * HALF : (h + 1) * HALF
+                ],
+                in_=rotated[:],
+            )
 
 
+        all_tiles = slice(0, TOKEN_TILES)
+        pair_tiles = [slice(2 * pair, 2 * pair + 2) for pair in range(TOKEN_PAIRS)]
+        for tiles in pair_tiles:
+            load_x(0, tiles)
         load_w(0)
-        load_x(0)
-        load_x(1)
+        load_x(1, all_tiles)
         load_w(1)
 
         bias_bf16 = []
@@ -249,43 +281,58 @@ def tile_ropemultiheadattention_pa_kernel(tc, x, Wq, bq, Wk, bk, out_0, out_1):
         nc.vector.memset(zero[:], 0.0)
         nc.scalar.activation(out=warm[:], in_=zero[:], func=ACT.Sin)
 
-        make_identity(nc, identity[:])
         nc.gpsimd.iota(
-            token[:],
-            pattern=[[1, TOKEN_TILES], [TOKEN_TILES, P]],
+            token[:, 0, :],
+            pattern=[[TOKEN_TILES, P]],
             base=0,
             channel_multiplier=0,
             allow_small_or_imprecise_dtypes=True,
         )
+        for r in range(1, TOKEN_TILES):
+            nc.vector.tensor_scalar_add(out=token[:, r, :], in0=token[:, 0, :], scalar1=float(r))
+        base = keep.tile([P, HALVES], F32)
+        index = keep.tile([P, HALVES], F32)
+        exponent = keep.tile([P, HALVES], F32)
+        nc.vector.memset(base[:], ROPE_BASE)
+        nc.gpsimd.iota(
+            index[:],
+            pattern=[[P, HALVES]],
+            base=0,
+            channel_multiplier=1,
+            allow_small_or_imprecise_dtypes=True,
+        )
+        nc.gpsimd.tensor_scalar(
+            out=exponent[:],
+            in0=index[:],
+            scalar1=-1.0 / FREQS,
+            scalar2=0.0,
+            op0=ALU.mult,
+            op1=ALU.add,
+        )
+        nc.gpsimd.tensor_tensor(out=freq[:], in0=base[:], in1=exponent[:], op=ALU.pow)
+        make_identity(nc, identity[:])
+        nc.vector.tensor_scalar_add(out=half_pi[:], in0=zero[:], scalar1=math.pi / 2.0)
+        nc.vector.tensor_scalar_add(out=whole_pi[:], in0=zero[:], scalar1=math.pi)
+        nc.vector.tensor_scalar_mul(out=half_freq[:], in0=freq[:, 1:2], scalar1=0.5)
+        nc.vector.tensor_scalar_mul(out=minus_freq[:], in0=freq[:, 1:2], scalar1=-1.0)
+
+        lower_angles()
+        upper_half_sin()
+        upper_cos()
         for w in range(PROJECTIONS):
             bias.append(keep.tile([P, HALVES, PARITIES], F32, name="bias%d" % w))
             nc.gpsimd.tensor_copy(out=bias[w][:], in_=bias_bf16[w][:])
-
-        freq_row = keep.tile([P, FREQS], F32)
-        nc.vector.memset(freq_row[:, 0:1], 1.0)
-        done = 1
-        while done < FREQS:
-            nc.vector.tensor_scalar_mul(
-                out=freq_row[:, done : 2 * done], in0=freq_row[:, 0:done], scalar1=RATIO**done
-            )
-            done *= 2
-        nc.vector.tensor_scalar_add(out=half_pi[:], in0=zero[:], scalar1=math.pi / 2.0)
-
-        freq_flip = flip_psum.tile([P, HALVES, P], F32, tag="flip")
-        for h in range(HALVES):
-            nc.tensor.transpose(freq_flip[:, h, :], freq_row[:, h * P : (h + 1) * P], identity[:])
-        nc.vector.tensor_scalar_mul(out=freq[:], in0=freq_flip[:, :, 0], scalar1=TURNS_PER_RADIAN)
-
-        group_w(0)
         transpose_x(0)
-        transpose_x(1)
-        group_x(0)
-        for table_step in (angle_in_turns, round_turns, excess_of_turns):
-            for h in range(HALVES):
-                table_step(h)
-        size_of_excess(0)
-        sin_table(0)
-        cos_table(0)
+        for pair in range(TOKEN_PAIRS):
+            group_x(0, pair)
+        lower_sin()
+        group_w(nc.vector.tensor_copy, 0, 0)
+        quantise_x(0, pair_tiles[0])
+        quantise_w(0, 0)
+        quantise_x(0, pair_tiles[1])
+        lower_sizes()
+        quantised.add((0, 0))
+        quantised.add(0)
         steps = [
             (w, b, e)
             for w in range(PROJECTIONS)
@@ -293,16 +340,19 @@ def tile_ropemultiheadattention_pa_kernel(tc, x, Wq, bq, Wk, bk, out_0, out_1):
             for e in range(PARITIES)
         ]
         ahead = multiply(*steps[0])
-        size_of_excess(1)
-        sin_table(1)
-        cos_table(1)
-        group_x(1)
-        group_w(1)
+        transpose_x(1)
+        group_w(nc.scalar.copy, 0, 1)
+        lower_cos()
+        upper_sin()
+        for pair in range(TOKEN_PAIRS):
+            group_x(1, pair)
+        for e in range(PARITIES):
+            group_w(nc.scalar.copy, 1, e)
 
         back = {}
         for step, (w, b, e) in enumerate(steps):
             proj = ahead
-            if step + 1 < len(steps):
+            if 0 < step < len(steps) - 1:
                 ahead = multiply(*steps[step + 1])
             for h in range(HALVES):
                 if e == 0:
@@ -310,6 +360,21 @@ def tile_ropemultiheadattention_pa_kernel(tc, x, Wq, bq, Wk, bk, out_0, out_1):
                         back[h, pair] = flip_psum.tile(
                             [P, 2, PARITIES, P], F32, tag="flip", name="back"
                         )
-                rotate(w, e, h, proj, back)
+                if step == len(steps) - 1:
+                    continue
+                rotate(w, e, h, all_tiles, proj, back)
+                if step == 0 and h == 0:
+                    prepare(*steps[1])
+                    ahead = multiply(*steps[1])
                 if e == PARITIES - 1:
-                    store(w, b, h, back)
+                    for pair in range(TOKEN_PAIRS):
+                        store(nc.scalar.copy, w, b, h, pair, back)
+            if step + 2 < len(steps):
+                prepare(*steps[step + 2])
+
+        w, b, e = steps[-1]
+        for pair in range(TOKEN_PAIRS):
+            for h in range(HALVES):
+                rotate(w, e, h, pair_tiles[pair], proj, back)
+                last = pair == TOKEN_PAIRS - 1 and h == HALVES - 1
+                store(nc.vector.tensor_copy if last else nc.scalar.copy, w, b, h, pair, back)

@@ -2,7 +2,6 @@ import math
 from contextlib import ExitStack
 
 import concourse.mybir as mybir
-from concourse.masks import make_identity
 
 F32 = mybir.dt.float32
 BF16 = mybir.dt.bfloat16
@@ -25,6 +24,9 @@ HALVES = 2
 HALF = FEAT // HALVES
 PARITIES = 2
 FREQS = FEAT // 2
+LOWER, UPPER = range(HALVES)
+SHARED_TILES = 1
+VECTOR_TILES = TOKEN_TILES - SHARED_TILES
 COS = 0
 SIN = 1
 ROPE_BASE = 10000.0
@@ -42,7 +44,7 @@ def tile_ropemultiheadattention_pa_kernel(tc, x, Wq, bq, Wk, bk, out_0, out_1):
 
     with ExitStack() as ctx:
         keep = ctx.enter_context(tc.tile_pool(name="keep", bufs=1))
-        products = ctx.enter_context(tc.tile_pool(name="products", bufs=8))
+        products = ctx.enter_context(tc.tile_pool(name="products", bufs=6))
         results = ctx.enter_context(tc.tile_pool(name="results", bufs=6))
         proj_psum = ctx.enter_context(tc.psum_pool(name="proj_psum", bufs=4))
         flip_psum = ctx.enter_context(tc.psum_pool(name="flip_psum", bufs=4))
@@ -99,16 +101,25 @@ def tile_ropemultiheadattention_pa_kernel(tc, x, Wq, bq, Wk, bk, out_0, out_1):
         w_codes = keep.tile([P, PROJECTIONS, FEAT], U32, align_bytes=64)
         w_scales = keep.tile([P, PROJECTIONS, FEAT], U8, align_bytes=64)
 
-        def group_w(copy, w, e):
-            by_parity = w_raw[:, w].rearrange("p t (h m e) -> p e h m t", h=HALVES, e=PARITIES)
-            copy(out=w_grouped[:, w, e], in_=by_parity[:, e])
+        both_halves = slice(0, HALVES)
 
-        def quantise_w(w, e):
-            columns = slice(e * HALF, (e + 1) * HALF)
+        def gpsimd_copy(out, in_):
+            nc.gpsimd.tensor_scalar(
+                out=out, in0=in_, scalar1=1.0, scalar2=0.0, op0=ALU.mult, op1=ALU.add
+            )
+
+        def group_w(copy, w, e, halves):
+            by_parity = w_raw[:, w].rearrange("p t (h m e) -> p e h m t", h=HALVES, e=PARITIES)
+            copy(out=w_grouped[:, w, e, halves], in_=by_parity[:, e, halves])
+
+        def quantise_w(w, e, halves):
+            columns = slice(
+                (e * HALVES + halves.start) * P, (e * HALVES + halves.stop) * P
+            )
             nc.vector.quantize_mx(
                 out=w_codes[:, w, columns].bitcast(FP8X4),
                 scales=w_scales[:, w, columns],
-                in_=w_grouped[:, w, e].rearrange("p h m t -> p (h m t)"),
+                in_=w_grouped[:, w, e, halves].rearrange("p h m t -> p (h m t)"),
             )
 
         token = keep.tile([P, TOKEN_TILES, P], F32)
@@ -199,7 +210,7 @@ def tile_ropemultiheadattention_pa_kernel(tc, x, Wq, bq, Wk, bk, out_0, out_1):
 
         def prepare(w, b, e):
             if (w, e) not in quantised:
-                quantise_w(w, e)
+                quantise_w(w, e, both_halves)
                 quantised.add((w, e))
             if b not in quantised:
                 quantise_x(b, slice(0, TOKEN_TILES))
@@ -221,24 +232,60 @@ def tile_ropemultiheadattention_pa_kernel(tc, x, Wq, bq, Wk, bk, out_0, out_1):
                 )
             return proj
 
-        def rotate(w, e, h, tiles, proj, back):
-            tokens = slice(tiles.start * P, tiles.stop * P)
+        shared = {}
+
+        def share(step):
+            w, b, e = steps[step]
+            biased = products.tile([P, SHARED_TILES * P], F32, tag="biased")
+            nc.scalar.activation(
+                out=biased[:],
+                in_=projections[step][UPPER][:, VECTOR_TILES * P :],
+                func=ACT.Identity,
+                bias=bias[w][:, UPPER, e : e + 1],
+            )
+            shared[step] = []
+            for h, kind in ((LOWER, SIN), (UPPER, COS)):
+                product = products.tile([P, SEQ], F32, tag="shared_product")
+                nc.gpsimd.tensor_mul(
+                    out=product[:, VECTOR_TILES * P :],
+                    in0=biased[:],
+                    in1=tables[:, h, kind, VECTOR_TILES * P :],
+                )
+                shared[step].append(product)
+
+        def rotate(step, h, tiles, proj):
+            w, b, e = steps[step]
             summands = []
             for source, kind in ((1 - h, SIN), (h, COS)):
-                product = products.tile([P, SEQ], F32, tag="product")
-                nc.vector.scalar_tensor_tensor(
-                    out=product[:, tokens],
-                    in0=proj[source][:, tokens],
-                    scalar=bias[w][:, source, e : e + 1],
-                    in1=tables[:, h, kind, tokens],
-                    op0=ALU.add,
-                    op1=ALU.mult,
-                )
+                stop = tiles.stop
+                if source == UPPER and step in shared:
+                    product = shared[step][h]
+                    stop = min(stop, VECTOR_TILES)
+                else:
+                    product = products.tile([P, SEQ], F32, tag="product")
+                if tiles.start < stop:
+                    tokens = slice(tiles.start * P, stop * P)
+                    nc.vector.scalar_tensor_tensor(
+                        out=product[:, tokens],
+                        in0=proj[source][:, tokens],
+                        scalar=bias[w][:, source, e : e + 1],
+                        in1=tables[:, h, kind, tokens],
+                        op0=ALU.add,
+                        op1=ALU.mult,
+                    )
                 summands.append(product)
+            return summands
+
+        def new_back(tiles):
+            return flip_psum.tile(
+                [P, tiles.stop - tiles.start, PARITIES, P], F32, tag="flip", name="back"
+            )
+
+        def add_up(summands, e, tiles, back):
             for r in range(tiles.start, tiles.stop):
                 for product in summands:
                     nc.tensor.matmul(
-                        out=back[h, r // 2][:, r % 2, e, :],
+                        out=back[:, r - tiles.start, e, :],
                         lhsT=product[:, r * P : (r + 1) * P],
                         rhs=identity[:],
                         is_transpose=True,
@@ -246,15 +293,15 @@ def tile_ropemultiheadattention_pa_kernel(tc, x, Wq, bq, Wk, bk, out_0, out_1):
                         stop=product is summands[-1],
                     )
 
-        def store(copy, w, b, h, pair, back):
-            rotated = results.tile([P, 2, HALF], F32)
+        def store(copy, w, b, h, tiles, back):
+            rotated = results.tile([P, tiles.stop - tiles.start, HALF], F32)
             copy(
                 out=rotated[:].rearrange("c r (m e) -> c r m e", e=PARITIES),
-                in_=back[h, pair][:].rearrange("c r e m -> c r m e"),
+                in_=back[:].rearrange("c r e m -> c r m e"),
             )
             nc.sync.dma_start(
                 out=outs[w][b].rearrange("(c r) i -> c r i", r=TOKEN_TILES)[
-                    :, pair_tiles[pair], h * HALF : (h + 1) * HALF
+                    :, tiles, h * HALF : (h + 1) * HALF
                 ],
                 in_=rotated[:],
             )
@@ -281,6 +328,17 @@ def tile_ropemultiheadattention_pa_kernel(tc, x, Wq, bq, Wk, bk, out_0, out_1):
         nc.vector.memset(zero[:], 0.0)
         nc.scalar.activation(out=warm[:], in_=zero[:], func=ACT.Sin)
 
+        base = keep.tile([P, HALVES], F32)
+        index = keep.tile([P, HALVES], F32)
+        exponent = keep.tile([P, HALVES], F32)
+        nc.vector.memset(base[:], ROPE_BASE)
+        nc.gpsimd.iota(
+            index[:],
+            pattern=[[TOKEN_TILES * P, HALVES]],
+            base=0,
+            channel_multiplier=TOKEN_TILES,
+            allow_small_or_imprecise_dtypes=True,
+        )
         nc.gpsimd.iota(
             token[:, 0, :],
             pattern=[[TOKEN_TILES, P]],
@@ -288,29 +346,24 @@ def tile_ropemultiheadattention_pa_kernel(tc, x, Wq, bq, Wk, bk, out_0, out_1):
             channel_multiplier=0,
             allow_small_or_imprecise_dtypes=True,
         )
-        for r in range(1, TOKEN_TILES):
-            nc.vector.tensor_scalar_add(out=token[:, r, :], in0=token[:, 0, :], scalar1=float(r))
-        base = keep.tile([P, HALVES], F32)
-        index = keep.tile([P, HALVES], F32)
-        exponent = keep.tile([P, HALVES], F32)
-        nc.vector.memset(base[:], ROPE_BASE)
-        nc.gpsimd.iota(
-            index[:],
-            pattern=[[P, HALVES]],
-            base=0,
-            channel_multiplier=1,
-            allow_small_or_imprecise_dtypes=True,
-        )
         nc.gpsimd.tensor_scalar(
             out=exponent[:],
             in0=index[:],
-            scalar1=-1.0 / FREQS,
+            scalar1=-1.0 / (TOKEN_TILES * FREQS),
             scalar2=0.0,
             op0=ALU.mult,
             op1=ALU.add,
         )
         nc.gpsimd.tensor_tensor(out=freq[:], in0=base[:], in1=exponent[:], op=ALU.pow)
-        make_identity(nc, identity[:])
+        nc.vector.tensor_scalar(
+            out=identity[:],
+            in0=token[:, 0, :],
+            scalar1=index[:, 0:1],
+            scalar2=None,
+            op0=ALU.is_equal,
+        )
+        for r in range(1, TOKEN_TILES):
+            nc.vector.tensor_scalar_add(out=token[:, r, :], in0=token[:, 0, :], scalar1=float(r))
         nc.vector.tensor_scalar_add(out=half_pi[:], in0=zero[:], scalar1=math.pi / 2.0)
         nc.vector.tensor_scalar_add(out=whole_pi[:], in0=zero[:], scalar1=math.pi)
         nc.vector.tensor_scalar_mul(out=half_freq[:], in0=freq[:, 1:2], scalar1=0.5)
@@ -326,11 +379,14 @@ def tile_ropemultiheadattention_pa_kernel(tc, x, Wq, bq, Wk, bk, out_0, out_1):
         for pair in range(TOKEN_PAIRS):
             group_x(0, pair)
         lower_sin()
-        group_w(nc.vector.tensor_copy, 0, 0)
-        quantise_x(0, pair_tiles[0])
-        quantise_w(0, 0)
-        quantise_x(0, pair_tiles[1])
         lower_sizes()
+        lower_half, upper_half = (slice(h, h + 1) for h in range(HALVES))
+        quantise_x(0, pair_tiles[0])
+        group_w(nc.vector.tensor_copy, 0, 0, upper_half)
+        quantise_x(0, pair_tiles[1])
+        quantise_w(0, 0, upper_half)
+        group_w(nc.vector.tensor_copy, 0, 0, lower_half)
+        quantise_w(0, 0, lower_half)
         quantised.add((0, 0))
         quantised.add(0)
         steps = [
@@ -339,42 +395,53 @@ def tile_ropemultiheadattention_pa_kernel(tc, x, Wq, bq, Wk, bk, out_0, out_1):
             for b in range(BATCH)
             for e in range(PARITIES)
         ]
-        ahead = multiply(*steps[0])
+        projections = {0: multiply(*steps[0])}
+        group_w(nc.scalar.copy, 0, 1, both_halves)
+        prepare(*steps[1])
         transpose_x(1)
-        group_w(nc.scalar.copy, 0, 1)
+        projections[1] = multiply(*steps[1])
         lower_cos()
         upper_sin()
         for pair in range(TOKEN_PAIRS):
             group_x(1, pair)
         for e in range(PARITIES):
-            group_w(nc.scalar.copy, 1, e)
+            group_w(gpsimd_copy, 1, e, both_halves)
+        share(1)
 
         back = {}
-        for step, (w, b, e) in enumerate(steps):
-            proj = ahead
-            if 0 < step < len(steps) - 1:
-                ahead = multiply(*steps[step + 1])
+        for step, (w, b, e) in enumerate(steps[:-PARITIES]):
+            proj = projections.pop(step)
             for h in range(HALVES):
                 if e == 0:
-                    for pair in range(TOKEN_PAIRS):
-                        back[h, pair] = flip_psum.tile(
-                            [P, 2, PARITIES, P], F32, tag="flip", name="back"
-                        )
-                if step == len(steps) - 1:
-                    continue
-                rotate(w, e, h, all_tiles, proj, back)
-                if step == 0 and h == 0:
-                    prepare(*steps[1])
-                    ahead = multiply(*steps[1])
+                    back[h] = [new_back(tiles) for tiles in pair_tiles]
+                summands = rotate(step, h, all_tiles, proj)
+                if h == UPPER and step > 0:
+                    projections[step + 2] = multiply(*steps[step + 2])
+                    share(step + 2)
+                for tiles, sums in zip(pair_tiles, back[h]):
+                    add_up(summands, e, tiles, sums)
+                if step == 0 and h == UPPER:
+                    prepare(*steps[2])
+                    projections[2] = multiply(*steps[2])
+                    share(2)
+                elif step > 0 and h == LOWER:
+                    prepare(*steps[step + 2])
                 if e == PARITIES - 1:
-                    for pair in range(TOKEN_PAIRS):
-                        store(nc.scalar.copy, w, b, h, pair, back)
-            if step + 2 < len(steps):
-                prepare(*steps[step + 2])
+                    for tiles, sums in zip(pair_tiles, back[h]):
+                        store(nc.scalar.copy, w, b, h, tiles, sums)
 
-        w, b, e = steps[-1]
-        for pair in range(TOKEN_PAIRS):
-            for h in range(HALVES):
-                rotate(w, e, h, pair_tiles[pair], proj, back)
-                last = pair == TOKEN_PAIRS - 1 and h == HALVES - 1
-                store(nc.vector.tensor_copy if last else nc.scalar.copy, w, b, h, pair, back)
+        w, b, last_parity = steps[-1]
+        proj = [projections.pop(len(steps) - PARITIES + e) for e in range(PARITIES)]
+        single_tiles = [slice(r, r + 1) for r in (2, 3)]
+        for h, pieces in enumerate((pair_tiles, [pair_tiles[0]] + single_tiles)):
+            back = [new_back(tiles) for tiles in pieces]
+            summands = rotate(len(steps) - PARITIES, h, all_tiles, proj[0])
+            for tiles, sums in zip(pieces, back):
+                add_up(summands, 0, tiles, sums)
+            for tiles, sums in zip(pieces, back):
+                summands = rotate(len(steps) - 1, h, tiles, proj[last_parity])
+                add_up(summands, last_parity, tiles, sums)
+                if tiles not in single_tiles:
+                    store(nc.scalar.copy, w, b, h, tiles, sums)
+        for tiles, sums in zip(single_tiles, back[1:]):
+            store(nc.vector.tensor_copy, w, b, UPPER, tiles, sums)

@@ -51,6 +51,7 @@ def tile_ropemultiheadattention_pa_kernel(tc, x, Wq, bq, Wk, bk, out_0, out_1):
         ctx.enter_context(tc.manual_schedule())
 
 
+        both_halves = slice(0, HALVES)
         x_raw = keep.tile([P, BATCH, TOKEN_TILES, DIM], BF16)
         w_raw = keep.tile([P, PROJECTIONS, PACK, FEAT], BF16)
 
@@ -60,33 +61,32 @@ def tile_ropemultiheadattention_pa_kernel(tc, x, Wq, bq, Wk, bk, out_0, out_1):
                 in_=x[b].rearrange("(c r) k -> c r k", r=TOKEN_TILES)[:, tiles, :],
             )
 
-        def load_w(w):
+        def load_w(w, halves):
+            features = slice(halves.start * HALF, halves.stop * HALF)
             nc.sync.dma_start(
-                out=w_raw[:, w], in_=weights[w].rearrange("(p t) i -> p t i", t=PACK)
+                out=w_raw[:, w, :, features],
+                in_=weights[w].rearrange("(p t) i -> p t i", t=PACK)[:, :, features],
             )
 
         identity = keep.tile([P, P], F32)
-        x_flip = {}
         x_grouped = keep.tile([P, BATCH, TOKEN_TILES, P, PACK], BF16, align_bytes=64)
         x_codes = keep.tile([P, BATCH, SEQ], U32, align_bytes=64)
         x_scales = keep.tile([P, BATCH, SEQ], U8, align_bytes=64)
 
-        def transpose_x(b):
+        def transpose_x(b, tiles):
             x_words = x_raw[:, b].bitcast(F32)
-            for pair in range(TOKEN_PAIRS):
-                x_flip[b, pair] = flip_psum.tile([P, 2, 2, P], F32, tag="flip", name="x_flip")
-                for r2 in range(2):
-                    for u in range(2):
-                        nc.tensor.transpose(
-                            x_flip[b, pair][:, r2, u, :],
-                            x_words[:, 2 * pair + r2, u::2],
-                            identity[:],
-                        )
+            flip = flip_psum.tile([P, tiles.stop - tiles.start, 2, P], F32, tag="flip", name="flip")
+            for r in range(tiles.start, tiles.stop):
+                for u in range(2):
+                    nc.tensor.transpose(
+                        flip[:, r - tiles.start, u, :], x_words[:, r, u::2], identity[:]
+                    )
+            return flip
 
-        def group_x(b, pair):
+        def group_x(b, tiles, flip):
             nc.scalar.copy(
-                out=x_grouped[:, b, 2 * pair : 2 * pair + 2, :, :].bitcast(F32),
-                in_=x_flip[b, pair][:].rearrange("p r u c -> p r c u"),
+                out=x_grouped[:, b, tiles, :, :].bitcast(F32),
+                in_=flip[:].rearrange("p r u c -> p r c u"),
             )
 
         def quantise_x(b, tiles):
@@ -100,8 +100,6 @@ def tile_ropemultiheadattention_pa_kernel(tc, x, Wq, bq, Wk, bk, out_0, out_1):
         w_grouped = keep.tile([P, PROJECTIONS, PARITIES, HALVES, P, PACK], BF16, align_bytes=64)
         w_codes = keep.tile([P, PROJECTIONS, FEAT], U32, align_bytes=64)
         w_scales = keep.tile([P, PROJECTIONS, FEAT], U8, align_bytes=64)
-
-        both_halves = slice(0, HALVES)
 
         def gpsimd_copy(out, in_):
             nc.gpsimd.tensor_scalar(
@@ -121,6 +119,14 @@ def tile_ropemultiheadattention_pa_kernel(tc, x, Wq, bq, Wk, bk, out_0, out_1):
                 scales=w_scales[:, w, columns],
                 in_=w_grouped[:, w, e, halves].rearrange("p h m t -> p (h m t)"),
             )
+
+        warm_sums = proj_psum.tile([P, SEQ], F32, tag="proj", name="warm_sums")
+
+        def warm_up(passes):
+            for i in range(passes):
+                nc.tensor.matmul(
+                    out=warm_sums[:, :P], lhsT=identity[:], rhs=identity[:], start=True, stop=True
+                )
 
         token = keep.tile([P, TOKEN_TILES, P], F32)
         freq = keep.tile([P, HALVES], F32)
@@ -157,14 +163,7 @@ def tile_ropemultiheadattention_pa_kernel(tc, x, Wq, bq, Wk, bk, out_0, out_1):
             nc.vector.tensor_sub(out=excess[:], in0=whole[:], in1=turns[:])
 
         def lower_sizes():
-            nc.vector.scalar_tensor_tensor(
-                out=size[:],
-                in0=excess[:],
-                scalar=-1.0,
-                in1=excess[:],
-                op0=ALU.mult,
-                op1=ALU.max,
-            )
+            nc.scalar.activation(out=size[:], in_=excess[:], func=ACT.Abs)
 
         def lower_sin():
             nc.scalar.activation(
@@ -216,9 +215,13 @@ def tile_ropemultiheadattention_pa_kernel(tc, x, Wq, bq, Wk, bk, out_0, out_1):
                 quantise_x(b, slice(0, TOKEN_TILES))
                 quantised.add(b)
 
-        def multiply(w, b, e):
+        def sources(step):
+            return (UPPER, LOWER) if step == 0 else (LOWER, UPPER)
+
+        def multiply(step):
+            w, b, e = steps[step]
             proj = {}
-            for h in reversed(range(HALVES)):
+            for h in sources(step):
                 tile_cols = slice((e * HALVES + h) * P, (e * HALVES + h + 1) * P)
                 proj[h] = proj_psum.tile([P, SEQ], F32, tag="proj", name="proj")
                 nc.tensor.matmul_mx(
@@ -256,7 +259,8 @@ def tile_ropemultiheadattention_pa_kernel(tc, x, Wq, bq, Wk, bk, out_0, out_1):
         def rotate(step, h, tiles, proj):
             w, b, e = steps[step]
             summands = []
-            for source, kind in ((1 - h, SIN), (h, COS)):
+            for source in sources(step):
+                kind = COS if source == h else SIN
                 stop = tiles.stop
                 if source == UPPER and step in shared:
                     product = shared[step][h]
@@ -309,11 +313,14 @@ def tile_ropemultiheadattention_pa_kernel(tc, x, Wq, bq, Wk, bk, out_0, out_1):
 
         all_tiles = slice(0, TOKEN_TILES)
         pair_tiles = [slice(2 * pair, 2 * pair + 2) for pair in range(TOKEN_PAIRS)]
-        for tiles in pair_tiles:
+        single_tiles = [slice(r, r + 1) for r in range(TOKEN_TILES)]
+        lower_half, upper_half = (slice(h, h + 1) for h in range(HALVES))
+        for tiles in single_tiles:
             load_x(0, tiles)
-        load_w(0)
+        load_w(0, upper_half)
+        load_w(0, lower_half)
         load_x(1, all_tiles)
-        load_w(1)
+        load_w(1, both_halves)
 
         bias_bf16 = []
         for w in range(PROJECTIONS):
@@ -375,18 +382,19 @@ def tile_ropemultiheadattention_pa_kernel(tc, x, Wq, bq, Wk, bk, out_0, out_1):
         for w in range(PROJECTIONS):
             bias.append(keep.tile([P, HALVES, PARITIES], F32, name="bias%d" % w))
             nc.gpsimd.tensor_copy(out=bias[w][:], in_=bias_bf16[w][:])
-        transpose_x(0)
-        for pair in range(TOKEN_PAIRS):
-            group_x(0, pair)
+        warm_up(1)
+        for tiles in single_tiles:
+            group_x(0, tiles, transpose_x(0, tiles))
+        warm_up(5)
         lower_sin()
-        lower_sizes()
-        lower_half, upper_half = (slice(h, h + 1) for h in range(HALVES))
         quantise_x(0, pair_tiles[0])
         group_w(nc.vector.tensor_copy, 0, 0, upper_half)
         quantise_x(0, pair_tiles[1])
         quantise_w(0, 0, upper_half)
         group_w(nc.vector.tensor_copy, 0, 0, lower_half)
         quantise_w(0, 0, lower_half)
+        lower_sizes()
+        lower_cos()
         quantised.add((0, 0))
         quantised.add(0)
         steps = [
@@ -395,18 +403,14 @@ def tile_ropemultiheadattention_pa_kernel(tc, x, Wq, bq, Wk, bk, out_0, out_1):
             for b in range(BATCH)
             for e in range(PARITIES)
         ]
-        projections = {0: multiply(*steps[0])}
+        projections = {0: multiply(0)}
         group_w(nc.scalar.copy, 0, 1, both_halves)
-        prepare(*steps[1])
-        transpose_x(1)
-        projections[1] = multiply(*steps[1])
-        lower_cos()
+        x_flips = [transpose_x(1, tiles) for tiles in pair_tiles]
         upper_sin()
-        for pair in range(TOKEN_PAIRS):
-            group_x(1, pair)
+        for tiles, flip in zip(pair_tiles, x_flips):
+            group_x(1, tiles, flip)
         for e in range(PARITIES):
             group_w(gpsimd_copy, 1, e, both_halves)
-        share(1)
 
         back = {}
         for step, (w, b, e) in enumerate(steps[:-PARITIES]):
@@ -415,14 +419,18 @@ def tile_ropemultiheadattention_pa_kernel(tc, x, Wq, bq, Wk, bk, out_0, out_1):
                 if e == 0:
                     back[h] = [new_back(tiles) for tiles in pair_tiles]
                 summands = rotate(step, h, all_tiles, proj)
-                if h == UPPER and step > 0:
-                    projections[step + 2] = multiply(*steps[step + 2])
+                if step == 0 and h == LOWER:
+                    prepare(*steps[1])
+                    projections[1] = multiply(1)
+                    share(1)
+                elif step > 0 and h == UPPER:
+                    projections[step + 2] = multiply(step + 2)
                     share(step + 2)
                 for tiles, sums in zip(pair_tiles, back[h]):
                     add_up(summands, e, tiles, sums)
                 if step == 0 and h == UPPER:
                     prepare(*steps[2])
-                    projections[2] = multiply(*steps[2])
+                    projections[2] = multiply(2)
                     share(2)
                 elif step > 0 and h == LOWER:
                     prepare(*steps[step + 2])
@@ -432,8 +440,8 @@ def tile_ropemultiheadattention_pa_kernel(tc, x, Wq, bq, Wk, bk, out_0, out_1):
 
         w, b, last_parity = steps[-1]
         proj = [projections.pop(len(steps) - PARITIES + e) for e in range(PARITIES)]
-        single_tiles = [slice(r, r + 1) for r in (2, 3)]
-        for h, pieces in enumerate((pair_tiles, [pair_tiles[0]] + single_tiles)):
+        last_tiles = single_tiles[2:]
+        for h, pieces in enumerate((pair_tiles, [pair_tiles[0]] + last_tiles)):
             back = [new_back(tiles) for tiles in pieces]
             summands = rotate(len(steps) - PARITIES, h, all_tiles, proj[0])
             for tiles, sums in zip(pieces, back):
@@ -441,7 +449,7 @@ def tile_ropemultiheadattention_pa_kernel(tc, x, Wq, bq, Wk, bk, out_0, out_1):
             for tiles, sums in zip(pieces, back):
                 summands = rotate(len(steps) - 1, h, tiles, proj[last_parity])
                 add_up(summands, last_parity, tiles, sums)
-                if tiles not in single_tiles:
+                if tiles not in last_tiles:
                     store(nc.scalar.copy, w, b, h, tiles, sums)
-        for tiles, sums in zip(single_tiles, back[1:]):
+        for tiles, sums in zip(last_tiles, back[1:]):
             store(nc.vector.tensor_copy, w, b, UPPER, tiles, sums)

@@ -25,8 +25,6 @@ HALF = FEAT // HALVES
 PARITIES = 2
 FREQS = FEAT // 2
 LOWER, UPPER = range(HALVES)
-SHARED_TILES = 1
-VECTOR_TILES = TOKEN_TILES - SHARED_TILES
 COS = 0
 SIN = 1
 ROPE_BASE = 10000.0
@@ -44,7 +42,7 @@ def tile_ropemultiheadattention_pa_kernel(tc, x, Wq, bq, Wk, bk, out_0, out_1):
 
     with ExitStack() as ctx:
         keep = ctx.enter_context(tc.tile_pool(name="keep", bufs=1))
-        products = ctx.enter_context(tc.tile_pool(name="products", bufs=6))
+        products = ctx.enter_context(tc.tile_pool(name="products", bufs=8))
         results = ctx.enter_context(tc.tile_pool(name="results", bufs=6))
         proj_psum = ctx.enter_context(tc.psum_pool(name="proj_psum", bufs=4))
         flip_psum = ctx.enter_context(tc.psum_pool(name="flip_psum", bufs=4))
@@ -100,11 +98,6 @@ def tile_ropemultiheadattention_pa_kernel(tc, x, Wq, bq, Wk, bk, out_0, out_1):
         w_grouped = keep.tile([P, PROJECTIONS, PARITIES, HALVES, P, PACK], BF16, align_bytes=64)
         w_codes = keep.tile([P, PROJECTIONS, FEAT], U32, align_bytes=64)
         w_scales = keep.tile([P, PROJECTIONS, FEAT], U8, align_bytes=64)
-
-        def gpsimd_copy(out, in_):
-            nc.gpsimd.tensor_scalar(
-                out=out, in0=in_, scalar1=1.0, scalar2=0.0, op0=ALU.mult, op1=ALU.add
-            )
 
         def group_w(copy, w, e, halves):
             by_parity = w_raw[:, w].rearrange("p t (h m e) -> p e h m t", h=HALVES, e=PARITIES)
@@ -204,7 +197,8 @@ def tile_ropemultiheadattention_pa_kernel(tc, x, Wq, bq, Wk, bk, out_0, out_1):
                 op1=ALU.add,
             )
 
-        bias = []
+        bias_words = keep.tile([P, PROJECTIONS * HALVES], F32)
+        bias = bias_words[:].bitcast(BF16).rearrange("m (w h e) -> m w h e", w=PROJECTIONS, e=PARITIES)
         quantised = set()
 
         def prepare(w, b, e):
@@ -215,13 +209,10 @@ def tile_ropemultiheadattention_pa_kernel(tc, x, Wq, bq, Wk, bk, out_0, out_1):
                 quantise_x(b, slice(0, TOKEN_TILES))
                 quantised.add(b)
 
-        def sources(step):
-            return (UPPER, LOWER) if step == 0 else (LOWER, UPPER)
-
         def multiply(step):
             w, b, e = steps[step]
             proj = {}
-            for h in sources(step):
+            for h in (UPPER, LOWER):
                 tile_cols = slice((e * HALVES + h) * P, (e * HALVES + h + 1) * P)
                 proj[h] = proj_psum.tile([P, SEQ], F32, tag="proj", name="proj")
                 nc.tensor.matmul_mx(
@@ -235,48 +226,20 @@ def tile_ropemultiheadattention_pa_kernel(tc, x, Wq, bq, Wk, bk, out_0, out_1):
                 )
             return proj
 
-        shared = {}
-
-        def share(step):
-            w, b, e = steps[step]
-            biased = products.tile([P, SHARED_TILES * P], F32, tag="biased")
-            nc.scalar.activation(
-                out=biased[:],
-                in_=projections[step][UPPER][:, VECTOR_TILES * P :],
-                func=ACT.Identity,
-                bias=bias[w][:, UPPER, e : e + 1],
-            )
-            shared[step] = []
-            for h, kind in ((LOWER, SIN), (UPPER, COS)):
-                product = products.tile([P, SEQ], F32, tag="shared_product")
-                nc.gpsimd.tensor_mul(
-                    out=product[:, VECTOR_TILES * P :],
-                    in0=biased[:],
-                    in1=tables[:, h, kind, VECTOR_TILES * P :],
-                )
-                shared[step].append(product)
-
         def rotate(step, h, tiles, proj):
             w, b, e = steps[step]
+            tokens = slice(tiles.start * P, tiles.stop * P)
             summands = []
-            for source in sources(step):
-                kind = COS if source == h else SIN
-                stop = tiles.stop
-                if source == UPPER and step in shared:
-                    product = shared[step][h]
-                    stop = min(stop, VECTOR_TILES)
-                else:
-                    product = products.tile([P, SEQ], F32, tag="product")
-                if tiles.start < stop:
-                    tokens = slice(tiles.start * P, stop * P)
-                    nc.vector.scalar_tensor_tensor(
-                        out=product[:, tokens],
-                        in0=proj[source][:, tokens],
-                        scalar=bias[w][:, source, e : e + 1],
-                        in1=tables[:, h, kind, tokens],
-                        op0=ALU.add,
-                        op1=ALU.mult,
-                    )
+            for source in (UPPER, LOWER):
+                product = products.tile([P, SEQ], F32, tag="product")
+                nc.vector.scalar_tensor_tensor(
+                    out=product[:, tokens],
+                    in0=proj[source][:, tokens],
+                    scalar=bias[:, w, source, e : e + 1],
+                    in1=tables[:, h, COS if source == h else SIN, tokens],
+                    op0=ALU.add,
+                    op1=ALU.mult,
+                )
                 summands.append(product)
             return summands
 
@@ -317,18 +280,17 @@ def tile_ropemultiheadattention_pa_kernel(tc, x, Wq, bq, Wk, bk, out_0, out_1):
         lower_half, upper_half = (slice(h, h + 1) for h in range(HALVES))
         for tiles in single_tiles:
             load_x(0, tiles)
+        bias_rows = keep.tile([P, P], F32)
+        nc.vector.memset(bias_rows[:], 0.0)
+        for w in range(PROJECTIONS):
+            nc.sync.dma_start(
+                out=bias_rows[w * HALVES : (w + 1) * HALVES, :].bitcast(BF16),
+                in_=biases[w].rearrange("(h j) -> h j", h=HALVES),
+            )
         load_w(0, upper_half)
         load_w(0, lower_half)
         load_x(1, all_tiles)
         load_w(1, both_halves)
-
-        bias_bf16 = []
-        for w in range(PROJECTIONS):
-            bias_bf16.append(keep.tile([P, HALVES, PARITIES], BF16, name="bias_bf16_%d" % w))
-            nc.scalar.dma_start(
-                out=bias_bf16[w][:],
-                in_=biases[w].rearrange("(h m e) -> m h e", h=HALVES, e=PARITIES),
-            )
 
         zero = keep.tile([P, 1], F32)
         warm = keep.tile([P, 1], F32)
@@ -379,12 +341,12 @@ def tile_ropemultiheadattention_pa_kernel(tc, x, Wq, bq, Wk, bk, out_0, out_1):
         lower_angles()
         upper_half_sin()
         upper_cos()
-        for w in range(PROJECTIONS):
-            bias.append(keep.tile([P, HALVES, PARITIES], F32, name="bias%d" % w))
-            nc.gpsimd.tensor_copy(out=bias[w][:], in_=bias_bf16[w][:])
         warm_up(1)
         for tiles in single_tiles:
             group_x(0, tiles, transpose_x(0, tiles))
+        bias_flip = proj_psum.tile([P, P], F32, tag="proj", name="bias_flip")
+        nc.tensor.transpose(bias_flip[:], bias_rows[:], identity[:])
+        nc.scalar.copy(out=bias_words[:], in_=bias_flip[:, : PROJECTIONS * HALVES])
         warm_up(5)
         lower_sin()
         quantise_x(0, pair_tiles[0])
@@ -409,8 +371,6 @@ def tile_ropemultiheadattention_pa_kernel(tc, x, Wq, bq, Wk, bk, out_0, out_1):
         upper_sin()
         for tiles, flip in zip(pair_tiles, x_flips):
             group_x(1, tiles, flip)
-        for e in range(PARITIES):
-            group_w(gpsimd_copy, 1, e, both_halves)
 
         back = {}
         for step, (w, b, e) in enumerate(steps[:-PARITIES]):
@@ -421,18 +381,18 @@ def tile_ropemultiheadattention_pa_kernel(tc, x, Wq, bq, Wk, bk, out_0, out_1):
                 summands = rotate(step, h, all_tiles, proj)
                 if step == 0 and h == LOWER:
                     prepare(*steps[1])
-                    projections[1] = multiply(1)
-                    share(1)
                 elif step > 0 and h == UPPER:
                     projections[step + 2] = multiply(step + 2)
-                    share(step + 2)
                 for tiles, sums in zip(pair_tiles, back[h]):
                     add_up(summands, e, tiles, sums)
-                if step == 0 and h == UPPER:
+                if step == 0 and h == LOWER:
+                    projections[1] = multiply(1)
+                    for second_parity in range(PARITIES):
+                        group_w(nc.scalar.copy, 1, second_parity, both_halves)
+                elif step == 0:
                     prepare(*steps[2])
                     projections[2] = multiply(2)
-                    share(2)
-                elif step > 0 and h == LOWER:
+                elif h == LOWER:
                     prepare(*steps[step + 2])
                 if e == PARITIES - 1:
                     for tiles, sums in zip(pair_tiles, back[h]):

@@ -42,7 +42,7 @@ def tile_ropemultiheadattention_pa_kernel(tc, x, Wq, bq, Wk, bk, out_0, out_1):
 
     with ExitStack() as ctx:
         keep = ctx.enter_context(tc.tile_pool(name="keep", bufs=1))
-        products = ctx.enter_context(tc.tile_pool(name="products", bufs=8))
+        products = ctx.enter_context(tc.tile_pool(name="products", bufs=12))
         results = ctx.enter_context(tc.tile_pool(name="results", bufs=6))
         proj_psum = ctx.enter_context(tc.psum_pool(name="proj_psum", bufs=4))
         flip_psum = ctx.enter_context(tc.psum_pool(name="flip_psum", bufs=4))
@@ -59,11 +59,9 @@ def tile_ropemultiheadattention_pa_kernel(tc, x, Wq, bq, Wk, bk, out_0, out_1):
                 in_=x[b].rearrange("(c r) k -> c r k", r=TOKEN_TILES)[:, tiles, :],
             )
 
-        def load_w(w, halves):
-            features = slice(halves.start * HALF, halves.stop * HALF)
+        def load_w(w):
             nc.sync.dma_start(
-                out=w_raw[:, w, :, features],
-                in_=weights[w].rearrange("(p t) i -> p t i", t=PACK)[:, :, features],
+                out=w_raw[:, w], in_=weights[w].rearrange("(p t) i -> p t i", t=PACK)
             )
 
         identity = keep.tile([P, P], F32)
@@ -209,39 +207,43 @@ def tile_ropemultiheadattention_pa_kernel(tc, x, Wq, bq, Wk, bk, out_0, out_1):
                 quantise_x(b, slice(0, TOKEN_TILES))
                 quantised.add(b)
 
-        def multiply(step):
+        def multiply(step, tiles):
             w, b, e = steps[step]
+            tokens = slice(tiles.start * P, tiles.stop * P)
             proj = {}
             for h in (UPPER, LOWER):
                 tile_cols = slice((e * HALVES + h) * P, (e * HALVES + h + 1) * P)
-                proj[h] = proj_psum.tile([P, SEQ], F32, tag="proj", name="proj")
+                proj[h] = proj_psum.tile(
+                    [P, (tiles.stop - tiles.start) * P], F32, tag="proj", name="proj"
+                )
                 nc.tensor.matmul_mx(
                     out=proj[h][:],
                     lhsT=w_codes[:, w, tile_cols].bitcast(FP8X4),
                     lhsT_scale=w_scales[:, w, tile_cols],
-                    rhs=x_codes[:, b, :].bitcast(FP8X4),
-                    rhs_scale=x_scales[:, b, :],
+                    rhs=x_codes[:, b, tokens].bitcast(FP8X4),
+                    rhs_scale=x_scales[:, b, tokens],
                     start=True,
                     stop=True,
                 )
             return proj
 
-        def rotate(step, h, tiles, proj):
+        def multiply_by_table(step, h, source, tiles, proj):
             w, b, e = steps[step]
             tokens = slice(tiles.start * P, tiles.stop * P)
-            summands = []
-            for source in (UPPER, LOWER):
-                product = products.tile([P, SEQ], F32, tag="product")
-                nc.vector.scalar_tensor_tensor(
-                    out=product[:, tokens],
-                    in0=proj[source][:, tokens],
-                    scalar=bias[:, w, source, e : e + 1],
-                    in1=tables[:, h, COS if source == h else SIN, tokens],
-                    op0=ALU.add,
-                    op1=ALU.mult,
-                )
-                summands.append(product)
-            return summands
+            covers_all = proj[source].shape[-1] == SEQ
+            product = products.tile([P, SEQ], F32, tag="product")
+            nc.vector.scalar_tensor_tensor(
+                out=product[:, tokens],
+                in0=proj[source][:, tokens] if covers_all else proj[source][:],
+                scalar=bias[:, w, source, e : e + 1],
+                in1=tables[:, h, COS if source == h else SIN, tokens],
+                op0=ALU.add,
+                op1=ALU.mult,
+            )
+            return product
+
+        def rotate(step, h, tiles, proj):
+            return [multiply_by_table(step, h, source, tiles, proj) for source in (UPPER, LOWER)]
 
         def new_back(tiles):
             return flip_psum.tile(
@@ -278,8 +280,7 @@ def tile_ropemultiheadattention_pa_kernel(tc, x, Wq, bq, Wk, bk, out_0, out_1):
         pair_tiles = [slice(2 * pair, 2 * pair + 2) for pair in range(TOKEN_PAIRS)]
         single_tiles = [slice(r, r + 1) for r in range(TOKEN_TILES)]
         lower_half, upper_half = (slice(h, h + 1) for h in range(HALVES))
-        for tiles in single_tiles:
-            load_x(0, tiles)
+        load_x(0, pair_tiles[0])
         bias_rows = keep.tile([P, P], F32)
         nc.vector.memset(bias_rows[:], 0.0)
         for w in range(PROJECTIONS):
@@ -287,10 +288,10 @@ def tile_ropemultiheadattention_pa_kernel(tc, x, Wq, bq, Wk, bk, out_0, out_1):
                 out=bias_rows[w * HALVES : (w + 1) * HALVES, :].bitcast(BF16),
                 in_=biases[w].rearrange("(h j) -> h j", h=HALVES),
             )
-        load_w(0, upper_half)
-        load_w(0, lower_half)
+        load_w(0)
+        load_x(0, pair_tiles[1])
         load_x(1, all_tiles)
-        load_w(1, both_halves)
+        load_w(1)
 
         zero = keep.tile([P, 1], F32)
         warm = keep.tile([P, 1], F32)
@@ -341,59 +342,76 @@ def tile_ropemultiheadattention_pa_kernel(tc, x, Wq, bq, Wk, bk, out_0, out_1):
         lower_angles()
         upper_half_sin()
         upper_cos()
+        upper_sin()
         warm_up(1)
-        for tiles in single_tiles:
+        for tiles in single_tiles[:2]:
             group_x(0, tiles, transpose_x(0, tiles))
         bias_flip = proj_psum.tile([P, P], F32, tag="proj", name="bias_flip")
         nc.tensor.transpose(bias_flip[:], bias_rows[:], identity[:])
         nc.scalar.copy(out=bias_words[:], in_=bias_flip[:, : PROJECTIONS * HALVES])
-        warm_up(5)
+        warm_up(3)
         lower_sin()
-        quantise_x(0, pair_tiles[0])
+        lower_sizes()
         group_w(nc.vector.tensor_copy, 0, 0, upper_half)
-        quantise_x(0, pair_tiles[1])
+        quantise_x(0, pair_tiles[0])
         quantise_w(0, 0, upper_half)
         group_w(nc.vector.tensor_copy, 0, 0, lower_half)
         quantise_w(0, 0, lower_half)
-        lower_sizes()
-        lower_cos()
         quantised.add((0, 0))
         quantised.add(0)
+        for tiles in single_tiles[2:]:
+            group_x(0, tiles, transpose_x(0, tiles))
+        lower_cos()
+        group_w(nc.scalar.copy, 0, 1, both_halves)
         steps = [
             (w, b, e)
             for w in range(PROJECTIONS)
             for b in range(BATCH)
             for e in range(PARITIES)
         ]
-        projections = {0: multiply(0)}
-        group_w(nc.scalar.copy, 0, 1, both_halves)
-        x_flips = [transpose_x(1, tiles) for tiles in pair_tiles]
-        upper_sin()
-        for tiles, flip in zip(pair_tiles, x_flips):
-            group_x(1, tiles, flip)
 
+        pair_projections = [multiply(0, pair_tiles[0])]
+        pair_summands = []
+        for pair, tiles in enumerate(pair_tiles):
+            summands = [[], []]
+            for source in (UPPER, LOWER):
+                for h in range(HALVES):
+                    summands[h].append(
+                        multiply_by_table(0, h, source, tiles, pair_projections[pair])
+                    )
+                if source == UPPER and pair == 0:
+                    quantise_x(0, pair_tiles[1])
+                    pair_projections.append(multiply(0, pair_tiles[1]))
+                    x_flips = [transpose_x(1, x_tiles) for x_tiles in pair_tiles]
+                    for x_tiles, flip in zip(pair_tiles, x_flips):
+                        group_x(1, x_tiles, flip)
+                elif source == UPPER:
+                    prepare(*steps[1])
+                    projections = {1: multiply(1, all_tiles)}
+            pair_summands.append(summands)
+        for e in range(PARITIES):
+            group_w(nc.scalar.copy, 1, e, both_halves)
         back = {}
-        for step, (w, b, e) in enumerate(steps[:-PARITIES]):
+        for h in range(HALVES):
+            back[h] = [new_back(tiles) for tiles in pair_tiles]
+            for tiles, sums, summands in zip(pair_tiles, back[h], pair_summands):
+                add_up(summands[h], 0, tiles, sums)
+
+        for step in range(1, len(steps) - PARITIES):
+            w, b, e = steps[step]
             proj = projections.pop(step)
             for h in range(HALVES):
                 if e == 0:
                     back[h] = [new_back(tiles) for tiles in pair_tiles]
                 summands = rotate(step, h, all_tiles, proj)
-                if step == 0 and h == LOWER:
-                    prepare(*steps[1])
-                elif step > 0 and h == UPPER:
-                    projections[step + 2] = multiply(step + 2)
+                if h == LOWER:
+                    following = 2 if step == 1 else step + 2
+                    prepare(*steps[following])
+                if step == 1 or h == UPPER:
+                    following = step + 1 + h
+                    projections[following] = multiply(following, all_tiles)
                 for tiles, sums in zip(pair_tiles, back[h]):
                     add_up(summands, e, tiles, sums)
-                if step == 0 and h == LOWER:
-                    projections[1] = multiply(1)
-                    for second_parity in range(PARITIES):
-                        group_w(nc.scalar.copy, 1, second_parity, both_halves)
-                elif step == 0:
-                    prepare(*steps[2])
-                    projections[2] = multiply(2)
-                elif h == LOWER:
-                    prepare(*steps[step + 2])
                 if e == PARITIES - 1:
                     for tiles, sums in zip(pair_tiles, back[h]):
                         store(nc.scalar.copy, w, b, h, tiles, sums)
@@ -403,9 +421,11 @@ def tile_ropemultiheadattention_pa_kernel(tc, x, Wq, bq, Wk, bk, out_0, out_1):
         last_tiles = single_tiles[2:]
         for h, pieces in enumerate((pair_tiles, [pair_tiles[0]] + last_tiles)):
             back = [new_back(tiles) for tiles in pieces]
-            summands = rotate(len(steps) - PARITIES, h, all_tiles, proj[0])
-            for tiles, sums in zip(pieces, back):
-                add_up(summands, 0, tiles, sums)
+            for whole_pair in pair_tiles:
+                summands = rotate(len(steps) - PARITIES, h, whole_pair, proj[0])
+                for tiles, sums in zip(pieces, back):
+                    if whole_pair.start <= tiles.start < whole_pair.stop:
+                        add_up(summands, 0, tiles, sums)
             for tiles, sums in zip(pieces, back):
                 summands = rotate(len(steps) - 1, h, tiles, proj[last_parity])
                 add_up(summands, last_parity, tiles, sums)

@@ -25,6 +25,8 @@ HALF = FEAT // HALVES
 PARITIES = 2
 FREQS = FEAT // 2
 LOWER, UPPER = range(HALVES)
+SHARED_TILES = 1
+VECTOR_TILES = TOKEN_TILES - SHARED_TILES
 COS = 0
 SIN = 1
 ROPE_BASE = 10000.0
@@ -43,7 +45,7 @@ def tile_ropemultiheadattention_pa_kernel(tc, x, Wq, bq, Wk, bk, out_0, out_1):
     with ExitStack() as ctx:
         keep = ctx.enter_context(tc.tile_pool(name="keep", bufs=1))
         products = ctx.enter_context(tc.tile_pool(name="products", bufs=12))
-        results = ctx.enter_context(tc.tile_pool(name="results", bufs=6))
+        results = ctx.enter_context(tc.tile_pool(name="results", bufs=3))
         proj_psum = ctx.enter_context(tc.psum_pool(name="proj_psum", bufs=4))
         flip_psum = ctx.enter_context(tc.psum_pool(name="flip_psum", bufs=4))
         ctx.enter_context(tc.manual_schedule())
@@ -195,6 +197,7 @@ def tile_ropemultiheadattention_pa_kernel(tc, x, Wq, bq, Wk, bk, out_0, out_1):
                 op1=ALU.add,
             )
 
+        projections = {}
         bias_words = keep.tile([P, PROJECTIONS * HALVES], F32)
         bias = bias_words[:].bitcast(BF16).rearrange("m (w h e) -> m w h e", w=PROJECTIONS, e=PARITIES)
         quantised = set()
@@ -207,11 +210,14 @@ def tile_ropemultiheadattention_pa_kernel(tc, x, Wq, bq, Wk, bk, out_0, out_1):
                 quantise_x(b, slice(0, TOKEN_TILES))
                 quantised.add(b)
 
+        def sources(step):
+            return (UPPER, LOWER) if step == 0 else (LOWER, UPPER)
+
         def multiply(step, tiles):
             w, b, e = steps[step]
             tokens = slice(tiles.start * P, tiles.stop * P)
             proj = {}
-            for h in (UPPER, LOWER):
+            for h in sources(step):
                 tile_cols = slice((e * HALVES + h) * P, (e * HALVES + h + 1) * P)
                 proj[h] = proj_psum.tile(
                     [P, (tiles.stop - tiles.start) * P], F32, tag="proj", name="proj"
@@ -227,52 +233,88 @@ def tile_ropemultiheadattention_pa_kernel(tc, x, Wq, bq, Wk, bk, out_0, out_1):
                 )
             return proj
 
+        shared = {}
+
+        def share(step):
+            w, b, e = steps[step]
+            biased = products.tile([P, SHARED_TILES * P], F32, tag="biased")
+            nc.scalar.activation(
+                out=biased[:],
+                in_=projections[step][UPPER][:, VECTOR_TILES * P :],
+                func=ACT.Identity,
+                bias=bias[:, w, UPPER, e : e + 1],
+            )
+            shared[step] = products.tile(
+                [P, HALVES, SHARED_TILES * P], F32, tag="shared", name="shared"
+            )
+            nc.gpsimd.tensor_mul(
+                out=shared[step][:],
+                in0=biased[:].unsqueeze(1).to_broadcast([P, HALVES, SHARED_TILES * P]),
+                in1=tables[:].rearrange("p h k s -> p (h k) s")[:, SIN : SIN + 2, VECTOR_TILES * P :],
+            )
+
         def multiply_by_table(step, h, source, tiles, proj):
             w, b, e = steps[step]
-            tokens = slice(tiles.start * P, tiles.stop * P)
-            covers_all = proj[source].shape[-1] == SEQ
-            product = products.tile([P, SEQ], F32, tag="product")
-            nc.vector.scalar_tensor_tensor(
-                out=product[:, tokens],
-                in0=proj[source][:, tokens] if covers_all else proj[source][:],
-                scalar=bias[:, w, source, e : e + 1],
-                in1=tables[:, h, COS if source == h else SIN, tokens],
-                op0=ALU.add,
-                op1=ALU.mult,
-            )
-            return product
+            summand = {}
+            stop = tiles.stop
+            if source == UPPER and step in shared:
+                stop = min(stop, VECTOR_TILES)
+                for r in range(max(tiles.start, stop), tiles.stop):
+                    summand[r] = shared[step][:, h, (r - stop) * P : (r - stop + 1) * P]
+            if tiles.start < stop:
+                product = products.tile([P, SEQ], F32, tag="product")
+                tokens = slice(tiles.start * P, stop * P)
+                covers_all = proj[source].shape[-1] == SEQ
+                nc.vector.scalar_tensor_tensor(
+                    out=product[:, tokens],
+                    in0=proj[source][:, tokens] if covers_all else proj[source][:],
+                    scalar=bias[:, w, source, e : e + 1],
+                    in1=tables[:, h, COS if source == h else SIN, tokens],
+                    op0=ALU.add,
+                    op1=ALU.mult,
+                )
+                for r in range(tiles.start, stop):
+                    summand[r] = product[:, r * P : (r + 1) * P]
+            return summand
 
         def rotate(step, h, tiles, proj):
-            return [multiply_by_table(step, h, source, tiles, proj) for source in (UPPER, LOWER)]
+            return [multiply_by_table(step, h, source, tiles, proj) for source in sources(step)]
 
-        def new_back(tiles):
-            return flip_psum.tile(
-                [P, tiles.stop - tiles.start, PARITIES, P], F32, tag="flip", name="back"
-            )
+        def new_back():
+            return flip_psum.tile([P, 2, PARITIES, P], F32, tag="flip", name="back")
 
-        def add_up(summands, e, tiles, back):
-            for r in range(tiles.start, tiles.stop):
-                for product in summands:
-                    nc.tensor.matmul(
-                        out=back[:, r - tiles.start, e, :],
-                        lhsT=product[:, r * P : (r + 1) * P],
-                        rhs=identity[:],
-                        is_transpose=True,
-                        start=product is summands[0],
-                        stop=product is summands[-1],
-                    )
+        def add_up(summands, r, out):
+            for i, summand in enumerate(summands):
+                nc.tensor.matmul(
+                    out=out,
+                    lhsT=summand[r],
+                    rhs=identity[:],
+                    is_transpose=True,
+                    start=i == 0,
+                    stop=i == len(summands) - 1,
+                )
 
-        def store(copy, w, b, h, tiles, back):
-            rotated = results.tile([P, tiles.stop - tiles.start, HALF], F32)
-            copy(
-                out=rotated[:].rearrange("c r (m e) -> c r m e", e=PARITIES),
+        def new_result():
+            return results.tile([P, TOKEN_TILES, FEAT], F32, tag="result", name="result")
+
+        def copy_half(result, h, tiles, back):
+            nc.scalar.copy(
+                out=result[:, tiles, h * HALF : (h + 1) * HALF].rearrange(
+                    "c r (m e) -> c r m e", e=PARITIES
+                ),
                 in_=back[:].rearrange("c r e m -> c r m e"),
             )
+
+        def copy_row(copy, result, r, back):
+            copy(
+                out=result[:, r, :].rearrange("c (h m e) -> c h m e", h=HALVES, e=PARITIES),
+                in_=back[:].rearrange("c h e m -> c h m e"),
+            )
+
+        def store(w, b, tiles, result):
             nc.sync.dma_start(
-                out=outs[w][b].rearrange("(c r) i -> c r i", r=TOKEN_TILES)[
-                    :, tiles, h * HALF : (h + 1) * HALF
-                ],
-                in_=rotated[:],
+                out=outs[w][b].rearrange("(c r) i -> c r i", r=TOKEN_TILES)[:, tiles, :],
+                in_=result[:, tiles, :],
             )
 
 
@@ -387,22 +429,27 @@ def tile_ropemultiheadattention_pa_kernel(tc, x, Wq, bq, Wk, bk, out_0, out_1):
                         group_x(1, x_tiles, flip)
                 elif source == UPPER:
                     prepare(*steps[1])
-                    projections = {1: multiply(1, all_tiles)}
+                    projections[1] = multiply(1, all_tiles)
+                    share(1)
             pair_summands.append(summands)
         for e in range(PARITIES):
             group_w(nc.scalar.copy, 1, e, both_halves)
         back = {}
         for h in range(HALVES):
-            back[h] = [new_back(tiles) for tiles in pair_tiles]
-            for tiles, sums, summands in zip(pair_tiles, back[h], pair_summands):
-                add_up(summands[h], 0, tiles, sums)
+            back[h] = [new_back() for pair in range(TOKEN_PAIRS)]
+            for pair, summands in enumerate(pair_summands):
+                for r2 in range(2):
+                    add_up(summands[h], 2 * pair + r2, back[h][pair][:, r2, 0, :])
 
+        result = new_result()
         for step in range(1, len(steps) - PARITIES):
             w, b, e = steps[step]
             proj = projections.pop(step)
+            if e == 0:
+                result = new_result()
             for h in range(HALVES):
                 if e == 0:
-                    back[h] = [new_back(tiles) for tiles in pair_tiles]
+                    back[h] = [new_back() for pair in range(TOKEN_PAIRS)]
                 summands = rotate(step, h, all_tiles, proj)
                 if h == LOWER:
                     following = 2 if step == 1 else step + 2
@@ -410,26 +457,34 @@ def tile_ropemultiheadattention_pa_kernel(tc, x, Wq, bq, Wk, bk, out_0, out_1):
                 if step == 1 or h == UPPER:
                     following = step + 1 + h
                     projections[following] = multiply(following, all_tiles)
-                for tiles, sums in zip(pair_tiles, back[h]):
-                    add_up(summands, e, tiles, sums)
+                    share(following)
+                for r in range(TOKEN_TILES):
+                    add_up(summands, r, back[h][r // 2][:, r % 2, e, :])
                 if e == PARITIES - 1:
-                    for tiles, sums in zip(pair_tiles, back[h]):
-                        store(nc.scalar.copy, w, b, h, tiles, sums)
+                    for pair, tiles in enumerate(pair_tiles):
+                        copy_half(result, h, tiles, back[h][pair])
+                        if h == UPPER:
+                            store(w, b, tiles, result)
 
-        w, b, last_parity = steps[-1]
-        proj = [projections.pop(len(steps) - PARITIES + e) for e in range(PARITIES)]
-        last_tiles = single_tiles[2:]
-        for h, pieces in enumerate((pair_tiles, [pair_tiles[0]] + last_tiles)):
-            back = [new_back(tiles) for tiles in pieces]
-            for whole_pair in pair_tiles:
-                summands = rotate(len(steps) - PARITIES, h, whole_pair, proj[0])
-                for tiles, sums in zip(pieces, back):
-                    if whole_pair.start <= tiles.start < whole_pair.stop:
-                        add_up(summands, 0, tiles, sums)
-            for tiles, sums in zip(pieces, back):
-                summands = rotate(len(steps) - 1, h, tiles, proj[last_parity])
-                add_up(summands, last_parity, tiles, sums)
-                if tiles not in last_tiles:
-                    store(nc.scalar.copy, w, b, h, tiles, sums)
-        for tiles, sums in zip(last_tiles, back[1:]):
-            store(nc.vector.tensor_copy, w, b, UPPER, tiles, sums)
+        w, b, e = steps[-1]
+        last_steps = range(len(steps) - PARITIES, len(steps))
+        result = new_result()
+        first_pair = pair_tiles[0]
+        pair_back = [new_back() for h in range(HALVES)]
+        for e, step in enumerate(last_steps):
+            for h in range(HALVES):
+                summands = rotate(step, h, first_pair, projections[step])
+                for r in range(first_pair.start, first_pair.stop):
+                    add_up(summands, r, pair_back[h][:, r, e, :])
+        for h in range(HALVES):
+            copy_half(result, h, first_pair, pair_back[h])
+        store(w, b, first_pair, result)
+        for r in range(first_pair.stop, TOKEN_TILES):
+            row_back = new_back()
+            for e, step in enumerate(last_steps):
+                for h in range(HALVES):
+                    summands = rotate(step, h, single_tiles[r], projections[step])
+                    add_up(summands, r, row_back[:, h, e, :])
+            last = r == TOKEN_TILES - 1
+            copy_row(nc.vector.tensor_copy if last else nc.scalar.copy, result, r, row_back)
+            store(w, b, single_tiles[r], result)

@@ -124,15 +124,15 @@ def tile_ropemultiheadattention_pa_kernel(tc, x, Wq, bq, Wk, bk, out_0, out_1):
         token = keep.tile([P, TOKEN_TILES, P], F32)
         freq = keep.tile([P, HALVES], F32)
         minus_freq = keep.tile([P, 1], F32)
-        half_freq = keep.tile([P, 1], F32)
+        minus_half_pi = keep.tile([P, 1], F32)
+        minus_pi = keep.tile([P, 1], F32)
         half_pi = keep.tile([P, 1], F32)
         whole_pi = keep.tile([P, 1], F32)
         turns = keep.tile([P, SEQ], F32)
         whole = keep.tile([P, SEQ], F32)
         excess = keep.tile([P, SEQ], F32)
         size = keep.tile([P, SEQ], F32)
-        half_sin = keep.tile([P, SEQ], F32)
-        half_sin_squared = keep.tile([P, SEQ], F32)
+        distance = keep.tile([P, SEQ], F32)
         tables = keep.tile([P, HALVES, 2, SEQ], F32)
         tokens_in_row = token[:].rearrange("p r c -> p (r c)")
 
@@ -172,9 +172,16 @@ def tile_ropemultiheadattention_pa_kernel(tc, x, Wq, bq, Wk, bk, out_0, out_1):
                 bias=half_pi[:],
             )
 
-        def upper_half_sin():
+        def upper_cos():
             nc.scalar.activation(
-                out=half_sin[:], in_=tokens_in_row, func=ACT.Sin, scale=half_freq[:]
+                out=distance[:],
+                in_=tokens_in_row,
+                func=ACT.Abs,
+                scale=freq[:, 1:2],
+                bias=minus_pi[:],
+            )
+            nc.scalar.activation(
+                out=tables[:, 1, COS, :], in_=distance[:], func=ACT.Sin, bias=minus_half_pi[:]
             )
 
         def upper_sin():
@@ -184,17 +191,6 @@ def tile_ropemultiheadattention_pa_kernel(tc, x, Wq, bq, Wk, bk, out_0, out_1):
                 func=ACT.Sin,
                 scale=minus_freq[:],
                 bias=whole_pi[:],
-            )
-
-        def upper_cos():
-            nc.gpsimd.tensor_mul(out=half_sin_squared[:], in0=half_sin[:], in1=half_sin[:])
-            nc.gpsimd.tensor_scalar(
-                out=tables[:, 1, COS, :],
-                in0=half_sin_squared[:],
-                scalar1=-2.0,
-                scalar2=1.0,
-                op0=ALU.mult,
-                op1=ALU.add,
             )
 
         projections = {}
@@ -378,11 +374,11 @@ def tile_ropemultiheadattention_pa_kernel(tc, x, Wq, bq, Wk, bk, out_0, out_1):
             nc.vector.tensor_scalar_add(out=token[:, r, :], in0=token[:, 0, :], scalar1=float(r))
         nc.vector.tensor_scalar_add(out=half_pi[:], in0=zero[:], scalar1=math.pi / 2.0)
         nc.vector.tensor_scalar_add(out=whole_pi[:], in0=zero[:], scalar1=math.pi)
-        nc.vector.tensor_scalar_mul(out=half_freq[:], in0=freq[:, 1:2], scalar1=0.5)
+        nc.vector.tensor_scalar_add(out=minus_pi[:], in0=zero[:], scalar1=-math.pi)
+        nc.vector.tensor_scalar_add(out=minus_half_pi[:], in0=zero[:], scalar1=-math.pi / 2.0)
         nc.vector.tensor_scalar_mul(out=minus_freq[:], in0=freq[:, 1:2], scalar1=-1.0)
 
         lower_angles()
-        upper_half_sin()
         upper_cos()
         upper_sin()
         warm_up(1)

@@ -27,6 +27,8 @@ FREQS = FEAT // 2
 LOWER, UPPER = range(HALVES)
 SHARED_TILES = 1
 VECTOR_TILES = TOKEN_TILES - SHARED_TILES
+PRODUCTS = 52
+SHARES = 7
 COS = 0
 SIN = 1
 ROPE_BASE = 10000.0
@@ -44,8 +46,9 @@ def tile_ropemultiheadattention_pa_kernel(tc, x, Wq, bq, Wk, bk, out_0, out_1):
 
     with ExitStack() as ctx:
         keep = ctx.enter_context(tc.tile_pool(name="keep", bufs=1))
-        products = ctx.enter_context(tc.tile_pool(name="products", bufs=12))
-        results = ctx.enter_context(tc.tile_pool(name="results", bufs=3))
+        products = ctx.enter_context(tc.tile_pool(name="products", bufs=PRODUCTS))
+        shares = ctx.enter_context(tc.tile_pool(name="shares", bufs=SHARES))
+        results = ctx.enter_context(tc.tile_pool(name="results", bufs=PROJECTIONS * BATCH))
         proj_psum = ctx.enter_context(tc.psum_pool(name="proj_psum", bufs=4))
         flip_psum = ctx.enter_context(tc.psum_pool(name="flip_psum", bufs=4))
         ctx.enter_context(tc.manual_schedule())
@@ -233,14 +236,14 @@ def tile_ropemultiheadattention_pa_kernel(tc, x, Wq, bq, Wk, bk, out_0, out_1):
 
         def share(step):
             w, b, e = steps[step]
-            biased = products.tile([P, SHARED_TILES * P], F32, tag="biased")
+            biased = shares.tile([P, SHARED_TILES * P], F32, tag="biased")
             nc.scalar.activation(
                 out=biased[:],
                 in_=projections[step][UPPER][:, VECTOR_TILES * P :],
                 func=ACT.Identity,
                 bias=bias[:, w, UPPER, e : e + 1],
             )
-            shared[step] = products.tile(
+            shared[step] = shares.tile(
                 [P, HALVES, SHARED_TILES * P], F32, tag="shared", name="shared"
             )
             nc.gpsimd.tensor_mul(

@@ -25,8 +25,6 @@ HALF = FEAT // HALVES
 PARITIES = 2
 FREQS = FEAT // 2
 LOWER, UPPER = range(HALVES)
-SHARED_TILES = 1
-VECTOR_TILES = TOKEN_TILES - SHARED_TILES
 PRODUCTS = 52
 SHARES = 7
 COS = 0
@@ -212,7 +210,7 @@ def tile_ropemultiheadattention_pa_kernel(tc, x, Wq, bq, Wk, bk, out_0, out_1):
         def sources(step):
             return (UPPER, LOWER) if step == 0 else (LOWER, UPPER)
 
-        def multiply(step, tiles):
+        def multiply(step, tiles, waits_before=None):
             w, b, e = steps[step]
             tokens = slice(tiles.start * P, tiles.stop * P)
             proj = {}
@@ -221,6 +219,10 @@ def tile_ropemultiheadattention_pa_kernel(tc, x, Wq, bq, Wk, bk, out_0, out_1):
                 proj[h] = proj_psum.tile(
                     [P, (tiles.stop - tiles.start) * P], F32, tag="proj", name="proj"
                 )
+                if h == waits_before:
+                    nc.tensor.matmul(
+                        out=proj[h][:, :P], lhsT=identity[:], rhs=identity[:], start=True, stop=True
+                    )
                 nc.tensor.matmul_mx(
                     out=proj[h][:],
                     lhsT=w_codes[:, w, tile_cols].bitcast(FP8X4),
@@ -234,22 +236,27 @@ def tile_ropemultiheadattention_pa_kernel(tc, x, Wq, bq, Wk, bk, out_0, out_1):
 
         shared = {}
 
+        def shared_tiles(step):
+            return 2 if step >= len(steps) - PARITIES else 1
+
         def share(step):
             w, b, e = steps[step]
-            biased = shares.tile([P, SHARED_TILES * P], F32, tag="biased")
+            count = shared_tiles(step)
+            start = (TOKEN_TILES - count) * P
+            biased = shares.tile([P, count * P], F32, tag="biased")
             nc.scalar.activation(
                 out=biased[:],
-                in_=projections[step][UPPER][:, VECTOR_TILES * P :],
+                in_=projections[step][UPPER][:, start:],
                 func=ACT.Identity,
                 bias=bias[:, w, UPPER, e : e + 1],
             )
             shared[step] = shares.tile(
-                [P, HALVES, SHARED_TILES * P], F32, tag="shared", name="shared"
+                [P, HALVES, count * P], F32, tag="shared", name="shared"
             )
             nc.gpsimd.tensor_mul(
                 out=shared[step][:],
-                in0=biased[:].unsqueeze(1).to_broadcast([P, HALVES, SHARED_TILES * P]),
-                in1=tables[:].rearrange("p h k s -> p (h k) s")[:, SIN : SIN + 2, VECTOR_TILES * P :],
+                in0=biased[:].unsqueeze(1).to_broadcast([P, HALVES, count * P]),
+                in1=tables[:].rearrange("p h k s -> p (h k) s")[:, SIN : SIN + 2, start:],
             )
 
         def multiply_by_table(step, h, source, tiles, proj):
@@ -257,9 +264,10 @@ def tile_ropemultiheadattention_pa_kernel(tc, x, Wq, bq, Wk, bk, out_0, out_1):
             summand = {}
             stop = tiles.stop
             if source == UPPER and step in shared:
-                stop = min(stop, VECTOR_TILES)
-                for r in range(max(tiles.start, stop), tiles.stop):
-                    summand[r] = shared[step][:, h, (r - stop) * P : (r - stop + 1) * P]
+                first = TOKEN_TILES - shared_tiles(step)
+                stop = min(stop, first)
+                for r in range(max(tiles.start, first), tiles.stop):
+                    summand[r] = shared[step][:, h, (r - first) * P : (r - first + 1) * P]
             if tiles.start < stop:
                 product = products.tile([P, SEQ], F32, tag="product")
                 tokens = slice(tiles.start * P, stop * P)
@@ -411,7 +419,7 @@ def tile_ropemultiheadattention_pa_kernel(tc, x, Wq, bq, Wk, bk, out_0, out_1):
             for e in range(PARITIES)
         ]
 
-        pair_projections = [multiply(0, pair_tiles[0])]
+        pair_projections = [multiply(0, pair_tiles[0], waits_before=LOWER)]
         pair_summands = []
         for pair, tiles in enumerate(pair_tiles):
             summands = [[], []]
@@ -422,7 +430,7 @@ def tile_ropemultiheadattention_pa_kernel(tc, x, Wq, bq, Wk, bk, out_0, out_1):
                     )
                 if source == UPPER and pair == 0:
                     quantise_x(0, pair_tiles[1])
-                    pair_projections.append(multiply(0, pair_tiles[1]))
+                    pair_projections.append(multiply(0, pair_tiles[1], waits_before=UPPER))
                     x_flips = [transpose_x(1, x_tiles) for x_tiles in pair_tiles]
                     for x_tiles, flip in zip(pair_tiles, x_flips):
                         group_x(1, x_tiles, flip)

@@ -391,7 +391,6 @@ def tile_ropemultiheadattention_pa_kernel(tc, x, Wq, bq, Wk, bk, out_0, out_1):
 
         lower_angles()
         upper_cos()
-        upper_sin()
         warm_up(1)
         for tiles in single_tiles[:2]:
             group_x(0, tiles, transpose_x(0, tiles))
@@ -401,6 +400,7 @@ def tile_ropemultiheadattention_pa_kernel(tc, x, Wq, bq, Wk, bk, out_0, out_1):
         warm_up(3)
         lower_sin()
         lower_sizes()
+        upper_sin()
         group_w(nc.vector.tensor_copy, 0, 0, upper_half)
         quantise_x(0, pair_tiles[0])
         quantise_w(0, 0, upper_half)
@@ -437,7 +437,6 @@ def tile_ropemultiheadattention_pa_kernel(tc, x, Wq, bq, Wk, bk, out_0, out_1):
                 elif source == UPPER:
                     prepare(*steps[1])
                     projections[1] = multiply(1, all_tiles)
-                    share(1)
             pair_summands.append(summands)
         for e in range(PARITIES):
             group_w(nc.scalar.copy, 1, e, both_halves)
@@ -464,7 +463,8 @@ def tile_ropemultiheadattention_pa_kernel(tc, x, Wq, bq, Wk, bk, out_0, out_1):
                 if step == 1 or h == UPPER:
                     following = step + 1 + h
                     projections[following] = multiply(following, all_tiles)
-                    share(following)
+                    if following > 2:
+                        share(following)
                 for r in range(TOKEN_TILES):
                     add_up(summands, r, back[h][r // 2][:, r % 2, e, :])
                 if e == PARITIES - 1:

import math
from contextlib import ExitStack

import concourse.mybir as mybir

F32 = mybir.dt.float32
BF16 = mybir.dt.bfloat16
U32 = mybir.dt.uint32
U8 = mybir.dt.uint8
FP8X4 = mybir.dt.float8_e4m3fn_x4
ALU = mybir.AluOpType
ACT = mybir.ActivationFunctionType

P = 128
PACK = 4
BATCH = 2
SEQ = 512
DIM = 512
FEAT = 512
PROJECTIONS = 2
TOKEN_TILES = SEQ // P
TOKEN_PAIRS = TOKEN_TILES // 2
HALVES = 2
HALF = FEAT // HALVES
PARITIES = 2
FREQS = FEAT // 2
LOWER, UPPER = range(HALVES)
PRODUCTS = 52
SHARES = 7
COS = 0
SIN = 1
ROPE_BASE = 10000.0
TURNS_PER_RADIAN = 1.0 / (2.0 * math.pi)
ROUND_MAGIC = 1.5 * 2.0**23

FLOPS = 2 * BATCH * SEQ * DIM * PROJECTIONS * FEAT


def tile_ropemultiheadattention_pa_kernel(tc, x, Wq, bq, Wk, bk, out_0, out_1):
    nc = tc.nc
    weights = (Wq, Wk)
    biases = (bq, bk)
    outs = (out_0, out_1)

    with ExitStack() as ctx:
        keep = ctx.enter_context(tc.tile_pool(name="keep", bufs=1))
        products = ctx.enter_context(tc.tile_pool(name="products", bufs=PRODUCTS))
        shares = ctx.enter_context(tc.tile_pool(name="shares", bufs=SHARES))
        results = ctx.enter_context(tc.tile_pool(name="results", bufs=PROJECTIONS * BATCH))
        proj_psum = ctx.enter_context(tc.psum_pool(name="proj_psum", bufs=4))
        flip_psum = ctx.enter_context(tc.psum_pool(name="flip_psum", bufs=4))
        ctx.enter_context(tc.manual_schedule())


        both_halves = slice(0, HALVES)
        x_raw = keep.tile([P, BATCH, TOKEN_TILES, DIM], BF16)
        w_raw = keep.tile([P, PROJECTIONS, PACK, FEAT], BF16)

        def load_x(b, tiles):
            nc.sync.dma_start(
                out=x_raw[:, b, tiles, :],
                in_=x[b].rearrange("(c r) k -> c r k", r=TOKEN_TILES)[:, tiles, :],
            )

        def load_w(w):
            nc.sync.dma_start(
                out=w_raw[:, w], in_=weights[w].rearrange("(p t) i -> p t i", t=PACK)
            )

        identity = keep.tile([P, P], F32)
        x_grouped = keep.tile([P, BATCH, TOKEN_TILES, P, PACK], BF16, align_bytes=64)
        x_codes = keep.tile([P, BATCH, SEQ], U32, align_bytes=64)
        x_scales = keep.tile([P, BATCH, SEQ], U8, align_bytes=64)

        def transpose_x(b, tiles):
            x_words = x_raw[:, b].bitcast(F32)
            flip = flip_psum.tile([P, tiles.stop - tiles.start, 2, P], F32, tag="flip", name="flip")
            for r in range(tiles.start, tiles.stop):
                for u in range(2):
                    nc.tensor.transpose(
                        flip[:, r - tiles.start, u, :], x_words[:, r, u::2], identity[:]
                    )
            return flip

        def group_x(b, tiles, flip):
            nc.scalar.copy(
                out=x_grouped[:, b, tiles, :, :].bitcast(F32),
                in_=flip[:].rearrange("p r u c -> p r c u"),
            )

        def quantise_x(b, tiles):
            tokens = slice(tiles.start * P, tiles.stop * P)
            nc.vector.quantize_mx(
                out=x_codes[:, b, tokens].bitcast(FP8X4),
                scales=x_scales[:, b, tokens],
                in_=x_grouped[:, b, tiles].rearrange("p r c t -> p (r c t)"),
            )

        w_grouped = keep.tile([P, PROJECTIONS, PARITIES, HALVES, P, PACK], BF16, align_bytes=64)
        w_codes = keep.tile([P, PROJECTIONS, FEAT], U32, align_bytes=64)
        w_scales = keep.tile([P, PROJECTIONS, FEAT], U8, align_bytes=64)

        def group_w(copy, w, e, halves):
            by_parity = w_raw[:, w].rearrange("p t (h m e) -> p e h m t", h=HALVES, e=PARITIES)
            copy(out=w_grouped[:, w, e, halves], in_=by_parity[:, e, halves])

        def quantise_w(w, e, halves):
            columns = slice(
                (e * HALVES + halves.start) * P, (e * HALVES + halves.stop) * P
            )
            nc.vector.quantize_mx(
                out=w_codes[:, w, columns].bitcast(FP8X4),
                scales=w_scales[:, w, columns],
                in_=w_grouped[:, w, e, halves].rearrange("p h m t -> p (h m t)"),
            )

        warm_sums = proj_psum.tile([P, SEQ], F32, tag="proj", name="warm_sums")

        def warm_up(passes):
            for i in range(passes):
                nc.tensor.matmul(
                    out=warm_sums[:, :P], lhsT=identity[:], rhs=identity[:], start=True, stop=True
                )

        token = keep.tile([P, TOKEN_TILES, P], F32)
        freq = keep.tile([P, HALVES], F32)
        minus_freq = keep.tile([P, 1], F32)
        minus_half_pi = keep.tile([P, 1], F32)
        minus_pi = keep.tile([P, 1], F32)
        half_pi = keep.tile([P, 1], F32)
        whole_pi = keep.tile([P, 1], F32)
        turns = keep.tile([P, SEQ], F32)
        whole = keep.tile([P, SEQ], F32)
        excess = keep.tile([P, SEQ], F32)
        size = keep.tile([P, SEQ], F32)
        distance = keep.tile([P, SEQ], F32)
        tables = keep.tile([P, HALVES, 2, SEQ], F32)
        tokens_in_row = token[:].rearrange("p r c -> p (r c)")

        def lower_angles():
            nc.vector.tensor_scalar(
                out=turns[:],
                in0=tokens_in_row,
                scalar1=freq[:, 0:1],
                scalar2=TURNS_PER_RADIAN,
                op0=ALU.mult,
                op1=ALU.mult,
            )
            nc.vector.tensor_scalar(
                out=whole[:],
                in0=turns[:],
                scalar1=ROUND_MAGIC,
                scalar2=ROUND_MAGIC,
                op0=ALU.add,
                op1=ALU.subtract,
            )
            nc.vector.tensor_sub(out=excess[:], in0=whole[:], in1=turns[:])

        def lower_sizes():
            nc.scalar.activation(out=size[:], in_=excess[:], func=ACT.Abs)

        def lower_sin():
            nc.scalar.activation(
                out=tables[:, 0, SIN, :], in_=excess[:], func=ACT.Sin, scale=2.0 * math.pi
            )

        def lower_cos():
            nc.scalar.activation(
                out=tables[:, 0, COS, :],
                in_=size[:],
                func=ACT.Sin,
                scale=-2.0 * math.pi,
                bias=half_pi[:],
            )

        def upper_cos():
            nc.scalar.activation(
                out=distance[:],
                in_=tokens_in_row,
                func=ACT.Abs,
                scale=freq[:, 1:2],
                bias=minus_pi[:],
            )
            nc.scalar.activation(
                out=tables[:, 1, COS, :], in_=distance[:], func=ACT.Sin, bias=minus_half_pi[:]
            )

        def upper_sin():
            nc.scalar.activation(
                out=tables[:, 1, SIN, :],
                in_=tokens_in_row,
                func=ACT.Sin,
                scale=minus_freq[:],
                bias=whole_pi[:],
            )

        projections = {}
        bias_words = keep.tile([P, PROJECTIONS * HALVES], F32)
        bias = bias_words[:].bitcast(BF16).rearrange("m (w h e) -> m w h e", w=PROJECTIONS, e=PARITIES)
        quantised = set()

        def prepare(w, b, e):
            if (w, e) not in quantised:
                quantise_w(w, e, both_halves)
                quantised.add((w, e))
            if b not in quantised:
                quantise_x(b, slice(0, TOKEN_TILES))
                quantised.add(b)

        def sources(step):
            return (UPPER, LOWER) if step == 0 else (LOWER, UPPER)

        def multiply(step, tiles, waits_before=None):
            w, b, e = steps[step]
            tokens = slice(tiles.start * P, tiles.stop * P)
            proj = {}
            for h in sources(step):
                tile_cols = slice((e * HALVES + h) * P, (e * HALVES + h + 1) * P)
                proj[h] = proj_psum.tile(
                    [P, (tiles.stop - tiles.start) * P], F32, tag="proj", name="proj"
                )
                if h == waits_before:
                    nc.tensor.matmul(
                        out=proj[h][:, :P], lhsT=identity[:], rhs=identity[:], start=True, stop=True
                    )
                nc.tensor.matmul_mx(
                    out=proj[h][:],
                    lhsT=w_codes[:, w, tile_cols].bitcast(FP8X4),
                    lhsT_scale=w_scales[:, w, tile_cols],
                    rhs=x_codes[:, b, tokens].bitcast(FP8X4),
                    rhs_scale=x_scales[:, b, tokens],
                    start=True,
                    stop=True,
                )
            return proj

        shared = {}

        def shared_tiles(step):
            return 2 if step >= len(steps) - PARITIES else 1

        def share(step):
            w, b, e = steps[step]
            count = shared_tiles(step)
            start = (TOKEN_TILES - count) * P
            biased = shares.tile([P, count * P], F32, tag="biased")
            nc.scalar.activation(
                out=biased[:],
                in_=projections[step][UPPER][:, start:],
                func=ACT.Identity,
                bias=bias[:, w, UPPER, e : e + 1],
            )
            shared[step] = shares.tile(
                [P, HALVES, count * P], F32, tag="shared", name="shared"
            )
            nc.gpsimd.tensor_mul(
                out=shared[step][:],
                in0=biased[:].unsqueeze(1).to_broadcast([P, HALVES, count * P]),
                in1=tables[:].rearrange("p h k s -> p (h k) s")[:, SIN : SIN + 2, start:],
            )

        def multiply_by_table(step, h, source, tiles, proj):
            w, b, e = steps[step]
            summand = {}
            stop = tiles.stop
            if source == UPPER and step in shared:
                first = TOKEN_TILES - shared_tiles(step)
                stop = min(stop, first)
                for r in range(max(tiles.start, first), tiles.stop):
                    summand[r] = shared[step][:, h, (r - first) * P : (r - first + 1) * P]
            if tiles.start < stop:
                product = products.tile([P, SEQ], F32, tag="product")
                tokens = slice(tiles.start * P, stop * P)
                covers_all = proj[source].shape[-1] == SEQ
                nc.vector.scalar_tensor_tensor(
                    out=product[:, tokens],
                    in0=proj[source][:, tokens] if covers_all else proj[source][:],
                    scalar=bias[:, w, source, e : e + 1],
                    in1=tables[:, h, COS if source == h else SIN, tokens],
                    op0=ALU.add,
                    op1=ALU.mult,
                )
                for r in range(tiles.start, stop):
                    summand[r] = product[:, r * P : (r + 1) * P]
            return summand

        def rotate(step, h, tiles, proj):
            return [multiply_by_table(step, h, source, tiles, proj) for source in sources(step)]

        def new_back():
            return flip_psum.tile([P, 2, PARITIES, P], F32, tag="flip", name="back")

        def add_up(summands, r, out):
            for i, summand in enumerate(summands):
                nc.tensor.matmul(
                    out=out,
                    lhsT=summand[r],
                    rhs=identity[:],
                    is_transpose=True,
                    start=i == 0,
                    stop=i == len(summands) - 1,
                )

        def new_result():
            return results.tile([P, TOKEN_TILES, FEAT], F32, tag="result", name="result")

        def copy_half(result, h, tiles, back):
            nc.scalar.copy(
                out=result[:, tiles, h * HALF : (h + 1) * HALF].rearrange(
                    "c r (m e) -> c r m e", e=PARITIES
                ),
                in_=back[:].rearrange("c r e m -> c r m e"),
            )

        def copy_row(copy, result, r, back):
            copy(
                out=result[:, r, :].rearrange("c (h m e) -> c h m e", h=HALVES, e=PARITIES),
                in_=back[:].rearrange("c h e m -> c h m e"),
            )

        def store(w, b, tiles, result):
            nc.sync.dma_start(
                out=outs[w][b].rearrange("(c r) i -> c r i", r=TOKEN_TILES)[:, tiles, :],
                in_=result[:, tiles, :],
            )


        all_tiles = slice(0, TOKEN_TILES)
        pair_tiles = [slice(2 * pair, 2 * pair + 2) for pair in range(TOKEN_PAIRS)]
        single_tiles = [slice(r, r + 1) for r in range(TOKEN_TILES)]
        lower_half, upper_half = (slice(h, h + 1) for h in range(HALVES))
        load_x(0, pair_tiles[0])
        bias_rows = keep.tile([P, P], F32)
        nc.vector.memset(bias_rows[:], 0.0)
        for w in range(PROJECTIONS):
            nc.sync.dma_start(
                out=bias_rows[w * HALVES : (w + 1) * HALVES, :].bitcast(BF16),
                in_=biases[w].rearrange("(h j) -> h j", h=HALVES),
            )
        load_w(0)
        load_x(0, pair_tiles[1])
        load_x(1, all_tiles)
        load_w(1)

        zero = keep.tile([P, 1], F32)
        warm = keep.tile([P, 1], F32)
        nc.vector.memset(zero[:], 0.0)
        nc.scalar.activation(out=warm[:], in_=zero[:], func=ACT.Sin)

        base = keep.tile([P, HALVES], F32)
        index = keep.tile([P, HALVES], F32)
        exponent = keep.tile([P, HALVES], F32)
        nc.vector.memset(base[:], ROPE_BASE)
        nc.gpsimd.iota(
            index[:],
            pattern=[[TOKEN_TILES * P, HALVES]],
            base=0,
            channel_multiplier=TOKEN_TILES,
            allow_small_or_imprecise_dtypes=True,
        )
        nc.gpsimd.iota(
            token[:, 0, :],
            pattern=[[TOKEN_TILES, P]],
            base=0,
            channel_multiplier=0,
            allow_small_or_imprecise_dtypes=True,
        )
        nc.gpsimd.tensor_scalar(
            out=exponent[:],
            in0=index[:],
            scalar1=-1.0 / (TOKEN_TILES * FREQS),
            scalar2=0.0,
            op0=ALU.mult,
            op1=ALU.add,
        )
        nc.gpsimd.tensor_tensor(out=freq[:], in0=base[:], in1=exponent[:], op=ALU.pow)
        nc.vector.tensor_scalar(
            out=identity[:],
            in0=token[:, 0, :],
            scalar1=index[:, 0:1],
            scalar2=None,
            op0=ALU.is_equal,
        )
        for r in range(1, TOKEN_TILES):
            nc.vector.tensor_scalar_add(out=token[:, r, :], in0=token[:, 0, :], scalar1=float(r))
        nc.vector.tensor_scalar_add(out=half_pi[:], in0=zero[:], scalar1=math.pi / 2.0)
        nc.vector.tensor_scalar_add(out=whole_pi[:], in0=zero[:], scalar1=math.pi)
        nc.vector.tensor_scalar_add(out=minus_pi[:], in0=zero[:], scalar1=-math.pi)
        nc.vector.tensor_scalar_add(out=minus_half_pi[:], in0=zero[:], scalar1=-math.pi / 2.0)
        nc.vector.tensor_scalar_mul(out=minus_freq[:], in0=freq[:, 1:2], scalar1=-1.0)

        lower_angles()
        upper_cos()
        warm_up(1)
        for tiles in single_tiles[:2]:
            group_x(0, tiles, transpose_x(0, tiles))
        bias_flip = proj_psum.tile([P, P], F32, tag="proj", name="bias_flip")
        nc.tensor.transpose(bias_flip[:], bias_rows[:], identity[:])
        nc.scalar.copy(out=bias_words[:], in_=bias_flip[:, : PROJECTIONS * HALVES])
        warm_up(3)
        lower_sin()
        lower_sizes()
        upper_sin()
        group_w(nc.vector.tensor_copy, 0, 0, upper_half)
        quantise_x(0, pair_tiles[0])
        quantise_w(0, 0, upper_half)
        group_w(nc.vector.tensor_copy, 0, 0, lower_half)
        quantise_w(0, 0, lower_half)
        quantised.add((0, 0))
        quantised.add(0)
        for tiles in single_tiles[2:]:
            group_x(0, tiles, transpose_x(0, tiles))
        lower_cos()
        group_w(nc.scalar.copy, 0, 1, both_halves)
        steps = [
            (w, b, e)
            for w in range(PROJECTIONS)
            for b in range(BATCH)
            for e in range(PARITIES)
        ]

        pair_projections = [multiply(0, pair_tiles[0], waits_before=LOWER)]
        pair_summands = []
        for pair, tiles in enumerate(pair_tiles):
            summands = [[], []]
            for source in (UPPER, LOWER):
                for h in range(HALVES):
                    summands[h].append(
                        multiply_by_table(0, h, source, tiles, pair_projections[pair])
                    )
                if source == UPPER and pair == 0:
                    quantise_x(0, pair_tiles[1])
                    pair_projections.append(multiply(0, pair_tiles[1], waits_before=UPPER))
                    x_flips = [transpose_x(1, x_tiles) for x_tiles in pair_tiles]
                    for x_tiles, flip in zip(pair_tiles, x_flips):
                        group_x(1, x_tiles, flip)
                elif source == UPPER:
                    prepare(*steps[1])
                    projections[1] = multiply(1, all_tiles)
            pair_summands.append(summands)
        for e in range(PARITIES):
            group_w(nc.scalar.copy, 1, e, both_halves)
        back = {}
        for h in range(HALVES):
            back[h] = [new_back() for pair in range(TOKEN_PAIRS)]
            for pair, summands in enumerate(pair_summands):
                for r2 in range(2):
                    add_up(summands[h], 2 * pair + r2, back[h][pair][:, r2, 0, :])

        result = new_result()
        for step in range(1, len(steps) - PARITIES):
            w, b, e = steps[step]
            proj = projections.pop(step)
            if e == 0:
                result = new_result()
            for h in range(HALVES):
                if e == 0:
                    back[h] = [new_back() for pair in range(TOKEN_PAIRS)]
                summands = rotate(step, h, all_tiles, proj)
                if h == LOWER:
                    following = 2 if step == 1 else step + 2
                    prepare(*steps[following])
                if step == 1 or h == UPPER:
                    following = step + 1 + h
                    projections[following] = multiply(following, all_tiles)
                    if following > 2:
                        share(following)
                for r in range(TOKEN_TILES):
                    add_up(summands, r, back[h][r // 2][:, r % 2, e, :])
                if e == PARITIES - 1:
                    for pair, tiles in enumerate(pair_tiles):
                        copy_half(result, h, tiles, back[h][pair])
                        if h == UPPER:
                            store(w, b, tiles, result)

        w, b, e = steps[-1]
        last_steps = range(len(steps) - PARITIES, len(steps))
        result = new_result()
        first_pair = pair_tiles[0]
        pair_back = [new_back() for h in range(HALVES)]
        for e, step in enumerate(last_steps):
            for h in range(HALVES):
                summands = rotate(step, h, first_pair, projections[step])
                for r in range(first_pair.start, first_pair.stop):
                    add_up(summands, r, pair_back[h][:, r, e, :])
        for h in range(HALVES):
            copy_half(result, h, first_pair, pair_back[h])
        store(w, b, first_pair, result)
        for r in range(first_pair.stop, TOKEN_TILES):
            row_back = new_back()
            for e, step in enumerate(last_steps):
                for h in range(HALVES):
                    summands = rotate(step, h, single_tiles[r], projections[step])
                    add_up(summands, r, row_back[:, h, e, :])
            last = r == TOKEN_TILES - 1
            copy_row(nc.vector.tensor_copy if last else nc.scalar.copy, result, r, row_back)
            store(w, b, single_tiles[r], result)
